import numpy as np
import ml_dtypes


def mxq(x, axis, fmt="e4m3"):
    dtype, down = {"e4m3": (ml_dtypes.float8_e4m3fn, 7), "e5m2": (ml_dtypes.float8_e5m2, 14)}[fmt]
    v = np.moveaxis(np.asarray(x, np.float32).astype(ml_dtypes.bfloat16).astype(np.float64), axis, -1)
    blocks = v.reshape(v.shape[:-1] + (-1, 32))
    amax = np.abs(blocks).max(-1, keepdims=True)
    byte = np.maximum(np.where(amax > 0, np.frexp(amax)[1] - 1 + 127, 0) - down, 1)
    scale = np.exp2(byte - 127.0)
    codes = (blocks / scale).astype(np.float32).astype(dtype).astype(np.float64)
    return np.moveaxis((codes * scale).reshape(v.shape), -1, axis)


WIDE = False


def mx_kscale(k):
    if not WIDE:
        return np.ones(k)
    levels = np.array([10, -10, 5, -5, 0])
    a = np.random.permutation(np.resize(levels, k // 512 * 4)).reshape(k // 512, 4)
    idx = np.arange(k)
    return np.exp2(a[idx // 512, idx % 128 // 32])


BF16 = ml_dtypes.bfloat16


def bf(x):
    return np.asarray(x, np.float32).astype(BF16)


def f64(x):
    return np.asarray(x).astype(np.float64)


E2M1 = np.array([0.0, 0.5, 1.0, 1.5, 2.0, 3.0, 4.0, 6.0, -0.0, -0.5, -1.0, -1.5, -2.0, -3.0, -4.0, -6.0])


def pack_weight(w, fmt):
    k, n = w.shape
    w = f64(bf(w)).reshape(k // 32, 32, n)
    amax = np.abs(w).max(1)
    if fmt == "e4m3":
        byte = np.frexp(amax)[1] - 1 + 127 - 7
    else:
        mant, ex = np.frexp(amax / 6.0)
        byte = np.where(mant > 0.5, ex, ex - 1) + 127
    byte = np.clip(np.where(amax > 0, byte, 1), 1, 254)
    scaled = (w * np.exp2(127.0 - byte)[:, None, :]).reshape(k, n).astype(np.float32)
    by_word = np.ascontiguousarray(scaled.reshape(k // 512, 128, 4, n).transpose(0, 1, 3, 2))
    if fmt == "e4m3":
        words = by_word.astype(ml_dtypes.float8_e4m3fn).view(np.uint8)
    else:
        c = by_word.astype(ml_dtypes.float4_e2m1fn).view(np.uint8) & 0xF
        words = c[..., 0::2] | (c[..., 1::2] << 4)
    return np.ascontiguousarray(words), np.ascontiguousarray(byte.astype(np.uint8).reshape(k // 512, 16, n))


def unpack_weight(words, scales, fmt):
    g, p, n, _ = words.shape
    if fmt == "e4m3":
        vals = np.ascontiguousarray(words).view(ml_dtypes.float8_e4m3fn).astype(np.float64)
    else:
        nib = np.empty((g, p, n, 4), np.uint8)
        nib[..., 0::2] = words & 0xF
        nib[..., 1::2] = words >> 4
        vals = E2M1[nib]
    vals = vals * np.repeat(np.exp2(scales.astype(np.float64) - 127.0), 8, axis=1)[..., None]
    return vals.transpose(0, 1, 3, 2).reshape(g * 512, n)

def pack4(w):
    words, scales = pack_weight(w, "e2m1")
    return words.reshape(words.shape[0], 128, -1), scales


def unpack4(words, scales):
    return unpack_weight(words.reshape(words.shape[0], 128, -1, 2), scales, "e2m1")


B, N, IN, H, D = 2, 64, 512, 8, 64
LN_EPS = 1e-5


def layer_norm(x, g, b):
    m = x.mean(-1, keepdims=True)
    v = ((x - m) ** 2).mean(-1, keepdims=True)
    return (x - m) / np.sqrt(v + LN_EPS) * g + b


def setup_inputs():
    t = mx_kscale(IN)
    u = np.concatenate([t, t, np.ones(IN)])
    keep = np.random.random((B, N)) < 0.9
    new_node = bf(np.random.standard_normal((B, N, IN)) * t)
    emb_edge = bf(np.random.standard_normal((B, N, N, IN)))
    node_mask = bf(keep * (0.5 + 0.5 * np.random.random((B, N))))
    words, scales = pack4(np.random.standard_normal((3 * IN, IN)) / np.sqrt(IN) / u[:, None])
    return {"new_node": new_node,
            "emb_edge": emb_edge,
            "node_mask": node_mask,
            "Wedge_words": words,
            "Wedge_scales": scales,
            "bedge": bf(np.random.standard_normal(IN) * 0.3),
            "gamma_e": bf(1.0 + 0.1 * np.random.standard_normal(IN)),
            "beta_e": bf(0.1 * np.random.standard_normal(IN))}


def reference(new_node, emb_edge, node_mask, Wedge_words, Wedge_scales, bedge, gamma_e, beta_e):
    x_mask = f64(node_mask)[..., None]
    e_mask = x_mask[:, :, None, :] * x_mask[:, None, :, :]
    xe = f64(emb_edge) * e_mask
    wq = unpack4(Wedge_words, Wedge_scales)
    nq = mxq(f64(new_node), 2, "e4m3")
    p_row = nq @ wq[:IN]
    p_col = nq @ wq[IN:IN + IN]
    p_edge = mxq(xe, 3, "e4m3") @ wq[IN + IN:]
    new_edge = p_row[:, :, None] + p_col[:, None] + p_edge + f64(bedge)
    return layer_norm(xe + new_edge, f64(gamma_e), f64(beta_e))

@@ -1,0 +1,369 @@
+import concourse.mybir as mybir
+from concourse.masks import make_identity
+
+F32 = mybir.dt.float32
+BF16 = mybir.dt.bfloat16
+I32 = mybir.dt.int32
+U32 = mybir.dt.uint32
+U8 = mybir.dt.uint8
+FP8X4 = mybir.dt.float8_e4m3fn_x4
+FP4X4 = mybir.dt.float4_e2m1fn_x4
+ALU = mybir.AluOpType
+ACT = mybir.ActivationFunctionType
+AXIS_X = mybir.AxisListType.X
+
+P = 128
+GRAPHS = 2
+NODES = 64
+FEAT = 512
+PACK = 4
+WORDS = FEAT // 2
+LN_EPS = 1e-5
+
+TILES = 4
+CHUNK_ROWS = P * TILES
+CHUNKS = GRAPHS * NODES * NODES // CHUNK_ROWS
+CHUNKS_PER_GRAPH = CHUNKS // GRAPHS
+I_PER_CHUNK = CHUNK_ROWS // NODES
+J_GROUPS = NODES // TILES
+
+ROW_BLOCK, COL_BLOCK, EDGE_BLOCK = 0, 1, 2
+
+FLOPS = 2 * FEAT * FEAT * (GRAPHS * NODES * NODES + 2 * GRAPHS * NODES)
+
+
+def tile_densegatlayer_pb_kernel(
+    tc, new_node, emb_edge, node_mask, Wedge_words, Wedge_scales, bedge, gamma_e, beta_e, out
+):
+    nc = tc.nc
+    emb_chunks = emb_edge.flatten_outer_dims().rearrange("(c p t) k -> c p t k", p=P, t=TILES)
+    out_chunks = out.flatten_outer_dims().rearrange("(c p t) k -> c p t k", p=P, t=TILES)
+
+    with (
+        tc.manual_schedule(),
+        tc.tile_pool(name="const", bufs=1) as const,
+        tc.tile_pool(name="emb", bufs=4) as emb_pool,
+        tc.tile_pool(name="stage", bufs=2) as stage,
+        tc.tile_pool(name="rows", bufs=4) as y_pool,
+        tc.tile_pool(name="stats", bufs=4) as stats,
+        tc.psum_pool(name="psum_const", bufs=1) as psum_const,
+        tc.psum_pool(name="psum_xt", bufs=2) as psum_xt,
+        tc.psum_pool(name="psum_acc", bufs=4) as psum_acc,
+    ):
+        w_planes = const.tile([P, 3, FEAT], U8, align_bytes=64)
+        nc.vector.memset(w_planes[:].bitcast(I32), 0)
+        w_words = const.tile([P, 3, 2 * FEAT], U8, align_bytes=64)
+
+        node_rows = const.tile([P, FEAT], BF16)
+        nc.sync.dma_start(out=node_rows[:], in_=new_node.flatten_outer_dims())
+
+        emb_tiles = {}
+
+        def load(c):
+            emb = emb_pool.tile([P, TILES, FEAT], BF16)
+            nc.sync.dma_start(out=emb[:], in_=emb_chunks[c])
+            emb_tiles[c] = emb
+
+        scales_i32 = Wedge_scales.bitcast(I32)
+        for quadrant in range(4):
+            nc.sync.dma_start(
+                out=w_planes[32 * quadrant : 32 * quadrant + 4].bitcast(I32),
+                in_=scales_i32[:, 4 * quadrant : 4 * quadrant + 4, :].rearrange("g q n -> q g n"),
+            )
+        nc.sync.dma_start(
+            out=w_words[:].bitcast(I32), in_=Wedge_words.bitcast(I32).rearrange("g p n -> p g n")
+        )
+
+        BIAS, GAMMA, BETA, MASK = 0, 1, 2, 3
+        vectors = const.tile([P, 4, FEAT], BF16)
+        nc.vector.memset(vectors[:], 0.0)
+        nc.scalar.dma_start(
+            out=vectors[0:1, MASK, 0 : GRAPHS * NODES],
+            in_=node_mask.rearrange("(o b) n -> o (b n)", o=1),
+        )
+        nc.scalar.dma_start(out=vectors[0:1, BIAS, :], in_=bedge.rearrange("(o n) -> o n", o=1))
+        nc.scalar.dma_start(out=vectors[0:1, GAMMA, :], in_=gamma_e.rearrange("(o n) -> o n", o=1))
+        nc.scalar.dma_start(out=vectors[0:1, BETA, :], in_=beta_e.rearrange("(o n) -> o n", o=1))
+        ones = const.tile([P, P], BF16)
+        nc.vector.memset(ones[:], 1.0)
+        eps = const.tile([P, 1], F32)
+        nc.vector.memset(eps[:], LN_EPS)
+        identity = const.tile([P, P], F32)
+        make_identity(nc, identity[:])
+
+        node_psum = psum_xt.tile([P, 2, 2, P], F32, tag="xt")
+        for u in range(2):
+            nc.tensor.transpose(
+                out=node_psum[:, 0, u, :],
+                in_=node_rows[:].bitcast(F32)[:, u:WORDS:2],
+                identity=identity[:],
+            )
+        node_words = const.tile([P, 2, P], F32)
+        nc.scalar.copy(out=node_words[:], in_=node_psum[:, 0, :, :])
+
+        def spread(psum_tile, which):
+            nc.tensor.matmul(
+                out=psum_tile[:], lhsT=ones[:], rhs=vectors[:, which, :], start=True, stop=True
+            )
+
+        mask_all = psum_acc.tile([P, FEAT], F32, tag="acc")
+        spread(mask_all, MASK)
+        bias_all = psum_const.tile([P, FEAT], F32)
+        spread(bias_all, BIAS)
+        gamma_all = psum_const.tile([P, FEAT], F32)
+        spread(gamma_all, GAMMA)
+        beta_psum = psum_acc.tile([P, FEAT], F32, tag="acc")
+        spread(beta_psum, BETA)
+
+        is_i = const.tile([P, I_PER_CHUNK], F32)
+        nc.vector.tensor_reduce(
+            out=is_i[:],
+            in_=identity[:].rearrange("p (a g) -> p a g", g=J_GROUPS),
+            axis=AXIS_X,
+            op=ALU.add,
+        )
+        is_j = const.tile([P, J_GROUPS], F32)
+        nc.vector.tensor_reduce(
+            out=is_j[:],
+            in_=identity[:].rearrange("p (a g) -> p g a", g=J_GROUPS),
+            axis=AXIS_X,
+            op=ALU.add,
+        )
+        mask_values = mask_all[:, 0 : GRAPHS * NODES]
+        picked_i = const.tile([P, CHUNKS, I_PER_CHUNK], F32)
+        nc.vector.tensor_tensor(
+            out=picked_i[:],
+            in0=mask_values.rearrange("p (c a) -> p c a", a=I_PER_CHUNK),
+            in1=is_i[:].unsqueeze(1).to_broadcast([P, CHUNKS, I_PER_CHUNK]),
+            op=ALU.mult,
+        )
+        mask_i = const.tile([P, CHUNKS], F32)
+        nc.vector.tensor_reduce(out=mask_i[:], in_=picked_i[:], axis=AXIS_X, op=ALU.add)
+        picked_j = const.tile([P, GRAPHS * TILES, J_GROUPS], F32)
+        nc.vector.tensor_tensor(
+            out=picked_j[:].rearrange("p (b t) g -> p b t g", t=TILES),
+            in0=mask_values.rearrange("p (b g t) -> p b t g", b=GRAPHS, t=TILES),
+            in1=is_j[:].unsqueeze(1).unsqueeze(1).to_broadcast([P, GRAPHS, TILES, J_GROUPS]),
+            op=ALU.mult,
+        )
+        mask_j = const.tile([P, GRAPHS * TILES], F32)
+        nc.vector.tensor_reduce(out=mask_j[:], in_=picked_j[:], axis=AXIS_X, op=ALU.add)
+        e_mask = const.tile([P, CHUNKS, TILES], F32)
+        nc.vector.tensor_tensor(
+            out=e_mask[:].rearrange("p (b c) t -> p b c t", b=GRAPHS),
+            in0=mask_i[:]
+            .rearrange("p (b c) -> p b c", b=GRAPHS)
+            .unsqueeze(3)
+            .to_broadcast([P, GRAPHS, CHUNKS_PER_GRAPH, TILES]),
+            in1=mask_j[:]
+            .rearrange("p (b t) -> p b t", b=GRAPHS)
+            .unsqueeze(2)
+            .to_broadcast([P, GRAPHS, CHUNKS_PER_GRAPH, TILES]),
+            op=ALU.mult,
+        )
+
+        beta_all = const.tile([P, FEAT], F32)
+        nc.vector.tensor_copy(out=beta_all[:], in_=beta_psum[:])
+        bias_sum = const.tile([P, 1], F32)
+        nc.vector.tensor_reduce(out=bias_sum[:], in_=bias_all[:], axis=AXIS_X, op=ALU.add)
+
+        row_codes = const.tile([P, GRAPHS, CHUNKS_PER_GRAPH * P], U32, align_bytes=64)
+        row_planes = const.tile([P, GRAPHS, CHUNKS_PER_GRAPH * P], U8, align_bytes=64)
+        col_codes = const.tile([P, GRAPHS, TILES * P], U32, align_bytes=64)
+        col_planes = const.tile([P, GRAPHS, TILES * P], U8, align_bytes=64)
+
+        def build_node_operands(b):
+            nodes = node_words[:, :, b * NODES : (b + 1) * NODES]
+            row_in = stage.tile([P, NODES * J_GROUPS * PACK], BF16, align_bytes=64)
+            nc.scalar.copy(
+                out=row_in[:].bitcast(F32).rearrange("p (n g u) -> p n g u", g=J_GROUPS, u=2),
+                in_=nodes.rearrange("p u n -> p n u")
+                .unsqueeze(2)
+                .to_broadcast([P, NODES, J_GROUPS, 2]),
+            )
+            col_in = stage.tile([P, TILES * P * PACK], BF16, align_bytes=64)
+            col_in_words = col_in[:].bitcast(F32).rearrange(
+                "p (t a g u) -> p t a g u", t=TILES, a=I_PER_CHUNK, u=2
+            )
+            for t in range(TILES):
+                nc.scalar.copy(
+                    out=col_in_words[:, t],
+                    in_=nodes[:, :, t:NODES:TILES]
+                    .rearrange("p u g -> p g u")
+                    .unsqueeze(1)
+                    .to_broadcast([P, I_PER_CHUNK, J_GROUPS, 2]),
+                )
+            nc.vector.quantize_mx(
+                out=row_codes[:, b, :].bitcast(FP8X4), scales=row_planes[:, b, :], in_=row_in[:]
+            )
+            nc.vector.quantize_mx(
+                out=col_codes[:, b, :].bitcast(FP8X4), scales=col_planes[:, b, :], in_=col_in[:]
+            )
+
+        xt_tiles, grouped_tiles, code_tiles, acc_tiles = {}, {}, {}, {}
+        y_tiles, sum_tiles, std_tiles = {}, {}, {}
+        squares_unread = const.tile([P, TILES, FEAT], BF16)
+
+        def mask_and_transpose(c):
+            emb = emb_tiles[c]
+            xe = stage.tile([P, TILES, FEAT], BF16)
+            for t in range(TILES):
+                nc.scalar.activation(
+                    out=xe[:, t, :], in_=emb[:, t, :], func=ACT.Copy, scale=e_mask[:, c, t : t + 1]
+                )
+            banks = []
+            for half in range(2):
+                xt = psum_xt.tile([P, 2, 2, P], F32, tag="xt")
+                for a in range(2):
+                    for u in range(2):
+                        nc.tensor.transpose(
+                            out=xt[:, a, u, :],
+                            in_=xe[:, 2 * half + a, :].bitcast(F32)[:, u:WORDS:2],
+                            identity=identity[:],
+                        )
+                banks.append(xt)
+            xt_tiles[c] = banks
+
+        def regroup(c):
+            grouped = stage.tile([P, TILES * P * PACK], BF16, align_bytes=64)
+            grouped_words = grouped[:].bitcast(F32).rearrange("p (t r u) -> p t r u", t=TILES, u=2)
+            for half in range(2):
+                nc.scalar.copy(
+                    out=grouped_words[:, 2 * half : 2 * half + 2],
+                    in_=xt_tiles[c][half][:].rearrange("p a u r -> p a r u"),
+                )
+            grouped_tiles[c] = grouped
+
+        def quantise(c):
+            codes = stage.tile([P, TILES * P], U32, align_bytes=64)
+            planes = stage.tile([P, TILES * P], U8, align_bytes=64)
+            nc.vector.quantize_mx(
+                out=codes[:].bitcast(FP8X4), scales=planes[:], in_=grouped_tiles[c][:]
+            )
+            code_tiles[c] = (codes, planes)
+
+        def multiply(c):
+            b, chunk_in_graph = divmod(c, CHUNKS_PER_GRAPH)
+            codes, planes = code_tiles[c]
+            row_cols = slice(chunk_in_graph * P, (chunk_in_graph + 1) * P)
+            accs = []
+            for t in range(TILES):
+                cols = slice(t * P, (t + 1) * P)
+                operands = (
+                    (ROW_BLOCK, row_codes[:, b, row_cols], row_planes[:, b, row_cols]),
+                    (COL_BLOCK, col_codes[:, b, cols], col_planes[:, b, cols]),
+                    (EDGE_BLOCK, codes[:, cols], planes[:, cols]),
+                )
+                acc = psum_acc.tile([P, FEAT], F32, tag="acc")
+                for block, lhs_codes, lhs_planes in operands:
+                    nc.tensor.matmul_mx(
+                        out=acc[:],
+                        lhsT=lhs_codes.bitcast(FP8X4),
+                        lhsT_scale=lhs_planes,
+                        rhs=w_words[:, block, :].bitcast(FP4X4),
+                        rhs_scale=w_planes[:, block, :],
+                        start=(block == ROW_BLOCK),
+                        stop=(block == EDGE_BLOCK),
+                    )
+                accs.append(acc)
+            acc_tiles[c] = accs
+
+        def add_residual(c):
+            y = y_pool.tile([P, TILES, FEAT], F32)
+            sums = stats.tile([P, TILES], F32)
+            for t in range(TILES):
+                nc.vector.scalar_tensor_tensor(
+                    out=y[:, t, :],
+                    in0=emb_tiles[c][:, t, :],
+                    scalar=e_mask[:, c, t : t + 1],
+                    in1=acc_tiles[c][t][:],
+                    op0=ALU.mult,
+                    op1=ALU.add,
+                    accum_out=sums[:, t : t + 1],
+                )
+            y_tiles[c] = y
+            sum_tiles[c] = sums
+
+        def centre(c):
+            y = y_tiles[c]
+            minus_mean = stats.tile([P, TILES], F32)
+            nc.vector.tensor_scalar(
+                out=minus_mean[:],
+                in0=sum_tiles[c][:],
+                scalar1=bias_sum[:, 0:1],
+                scalar2=-1.0 / FEAT,
+                op0=ALU.add,
+                op1=ALU.mult,
+            )
+            for t in range(TILES):
+                nc.vector.scalar_tensor_tensor(
+                    out=y[:, t, :],
+                    in0=y[:, t, :],
+                    scalar=minus_mean[:, t : t + 1],
+                    in1=bias_all[:],
+                    op0=ALU.add,
+                    op1=ALU.add,
+                )
+
+        def deviation(c):
+            y = y_tiles[c]
+            squares = stats.tile([P, TILES], F32)
+            for t in range(TILES):
+                nc.scalar.activation(
+                    out=squares_unread[:, t, :],
+                    in_=y[:, t, :],
+                    func=ACT.Square,
+                    accum_out=squares[:, t : t + 1],
+                )
+            std = stats.tile([P, TILES], F32)
+            nc.scalar.activation(
+                out=std[:], in_=squares[:], func=ACT.Sqrt, bias=eps[:, 0:1], scale=1.0 / FEAT
+            )
+            std_tiles[c] = std
+
+        def normalise(c):
+            y = y_tiles[c]
+            rstd = stats.tile([P, TILES], F32)
+            nc.vector.reciprocal(out=rstd[:], in_=std_tiles[c][:])
+            for t in range(TILES):
+                nc.vector.scalar_tensor_tensor(
+                    out=y[:, t, :],
+                    in0=y[:, t, :],
+                    scalar=rstd[:, t : t + 1],
+                    in1=gamma_all[:],
+                    op0=ALU.mult,
+                    op1=ALU.mult,
+                )
+
+        def shift_and_store(c):
+            y = y_tiles[c]
+            nc.gpsimd.tensor_tensor(
+                out=y[:],
+                in0=y[:],
+                in1=beta_all[:].unsqueeze(1).to_broadcast([P, TILES, FEAT]),
+                op=ALU.add,
+            )
+            nc.sync.dma_start(out=out_chunks[c], in_=y[:])
+
+        def live(c):
+            return 0 <= c < CHUNKS
+
+        for step in range(-2, CHUNKS + 3):
+            if live(step + 2):
+                load(step + 2)
+            if live(step + 1):
+                if (step + 1) % CHUNKS_PER_GRAPH == 0:
+                    build_node_operands((step + 1) // CHUNKS_PER_GRAPH)
+                mask_and_transpose(step + 1)
+            if live(step - 1):
+                add_residual(step - 1)
+                centre(step - 1)
+                deviation(step - 1)
+            if live(step + 1):
+                regroup(step + 1)
+            if live(step):
+                quantise(step)
+                multiply(step)
+            if live(step - 2):
+                normalise(step - 2)
+                shift_and_store(step - 2)

@@ -337,7 +337,7 @@ def tile_densegatlayer_pb_kernel(
 
         def shift_and_store(c):
             y = y_tiles[c]
-            nc.gpsimd.tensor_tensor(
+            nc.vector.tensor_tensor(
                 out=y[:],
                 in0=y[:],
                 in1=beta_all[:].unsqueeze(1).to_broadcast([P, TILES, FEAT]),

@@ -27,6 +27,7 @@ CHUNKS_PER_GRAPH = CHUNKS // GRAPHS
 I_PER_CHUNK = CHUNK_ROWS // NODES
 J_GROUPS = NODES // TILES
 
+FEATURE_BLOCKS = FEAT // P
 ROW_BLOCK, COL_BLOCK, EDGE_BLOCK = 0, 1, 2
 
 FLOPS = 2 * FEAT * FEAT * (GRAPHS * NODES * NODES + 2 * GRAPHS * NODES)
@@ -42,13 +43,13 @@ def tile_densegatlayer_pb_kernel(
     with (
         tc.manual_schedule(),
         tc.tile_pool(name="const", bufs=1) as const,
-        tc.tile_pool(name="emb", bufs=4) as emb_pool,
+        tc.tile_pool(name="emb", bufs=5) as emb_pool,
         tc.tile_pool(name="stage", bufs=2) as stage,
-        tc.tile_pool(name="rows", bufs=4) as y_pool,
+        tc.tile_pool(name="rows", bufs=3) as row_pool,
         tc.tile_pool(name="stats", bufs=4) as stats,
-        tc.psum_pool(name="psum_const", bufs=1) as psum_const,
         tc.psum_pool(name="psum_xt", bufs=2) as psum_xt,
-        tc.psum_pool(name="psum_acc", bufs=4) as psum_acc,
+        tc.psum_pool(name="psum_features", bufs=2) as psum_features,
+        tc.psum_pool(name="psum_rows", bufs=4) as psum_rows,
     ):
         w_planes = const.tile([P, 3, FEAT], U8, align_bytes=64)
         nc.vector.memset(w_planes[:].bitcast(I32), 0)
@@ -101,19 +102,17 @@ def tile_densegatlayer_pb_kernel(
         node_words = const.tile([P, 2, P], F32)
         nc.scalar.copy(out=node_words[:], in_=node_psum[:, 0, :, :])
 
-        def spread(psum_tile, which):
+        def spread(which):
+            psum_tile = psum_rows.tile([P, FEAT], F32, tag="by_rows")
             nc.tensor.matmul(
                 out=psum_tile[:], lhsT=ones[:], rhs=vectors[:, which, :], start=True, stop=True
             )
+            return psum_tile
 
-        mask_all = psum_acc.tile([P, FEAT], F32, tag="acc")
-        spread(mask_all, MASK)
-        bias_all = psum_const.tile([P, FEAT], F32)
-        spread(bias_all, BIAS)
-        gamma_all = psum_const.tile([P, FEAT], F32)
-        spread(gamma_all, GAMMA)
-        beta_psum = psum_acc.tile([P, FEAT], F32, tag="acc")
-        spread(beta_psum, BETA)
+        mask_all = spread(MASK)
+        bias_all = spread(BIAS)
+        gamma_psum = spread(GAMMA)
+        beta_psum = spread(BETA)
 
         is_i = const.tile([P, I_PER_CHUNK], F32)
         nc.vector.tensor_reduce(
@@ -162,10 +161,19 @@ def tile_densegatlayer_pb_kernel(
             op=ALU.mult,
         )
 
+        picked_bias = const.tile([P, FEATURE_BLOCKS, P], F32)
+        nc.vector.tensor_tensor(
+            out=picked_bias[:],
+            in0=bias_all[:].rearrange("p (f q) -> p f q", q=P),
+            in1=identity[:].unsqueeze(1).to_broadcast([P, FEATURE_BLOCKS, P]),
+            op=ALU.mult,
+        )
+        bias_column = const.tile([P, FEATURE_BLOCKS], F32)
+        nc.vector.tensor_reduce(out=bias_column[:], in_=picked_bias[:], axis=AXIS_X, op=ALU.add)
+        gamma_all = const.tile([P, FEAT], F32)
+        nc.vector.tensor_copy(out=gamma_all[:], in_=gamma_psum[:])
         beta_all = const.tile([P, FEAT], F32)
         nc.vector.tensor_copy(out=beta_all[:], in_=beta_psum[:])
-        bias_sum = const.tile([P, 1], F32)
-        nc.vector.tensor_reduce(out=bias_sum[:], in_=bias_all[:], axis=AXIS_X, op=ALU.add)
 
         row_codes = const.tile([P, GRAPHS, CHUNKS_PER_GRAPH * P], U32, align_bytes=64)
         row_planes = const.tile([P, GRAPHS, CHUNKS_PER_GRAPH * P], U8, align_bytes=64)
@@ -200,17 +208,26 @@ def tile_densegatlayer_pb_kernel(
                 out=col_codes[:, b, :].bitcast(FP8X4), scales=col_planes[:, b, :], in_=col_in[:]
             )
 
-        xt_tiles, grouped_tiles, code_tiles, acc_tiles = {}, {}, {}, {}
-        y_tiles, sum_tiles, std_tiles = {}, {}, {}
+        xe_tiles, xt_tiles, grouped_tiles, code_tiles, edge_tiles = {}, {}, {}, {}, {}
+        y_tiles, minus_mean_tiles, std_tiles, rstd_tiles, scaled_tiles = {}, {}, {}, {}, {}
         squares_unread = const.tile([P, TILES, FEAT], BF16)
 
-        def mask_and_transpose(c):
-            emb = emb_tiles[c]
+        def mask(c):
             xe = stage.tile([P, TILES, FEAT], BF16)
-            for t in range(TILES):
+            for t in range(0, TILES, 2):
                 nc.scalar.activation(
-                    out=xe[:, t, :], in_=emb[:, t, :], func=ACT.Copy, scale=e_mask[:, c, t : t + 1]
+                    out=xe[:, t, :],
+                    in_=emb_tiles[c][:, t, :],
+                    func=ACT.Copy,
+                    scale=e_mask[:, c, t : t + 1],
                 )
+            for t in range(1, TILES, 2):
+                nc.vector.tensor_scalar_mul(
+                    out=xe[:, t, :], in0=emb_tiles[c][:, t, :], scalar1=e_mask[:, c, t : t + 1]
+                )
+            xe_tiles[c] = xe
+
+        def transpose(c):
             banks = []
             for half in range(2):
                 xt = psum_xt.tile([P, 2, 2, P], F32, tag="xt")
@@ -218,7 +235,7 @@ def tile_densegatlayer_pb_kernel(
                     for u in range(2):
                         nc.tensor.transpose(
                             out=xt[:, a, u, :],
-                            in_=xe[:, 2 * half + a, :].bitcast(F32)[:, u:WORDS:2],
+                            in_=xe_tiles[c][:, 2 * half + a, :].bitcast(F32)[:, u:WORDS:2],
                             identity=identity[:],
                         )
                 banks.append(xt)
@@ -242,77 +259,103 @@ def tile_densegatlayer_pb_kernel(
             )
             code_tiles[c] = (codes, planes)
 
+        def weight(block, f):
+            return {
+                "lhsT": w_words[:, block, 2 * P * f : 2 * P * (f + 1)].bitcast(FP4X4),
+                "lhsT_scale": w_planes[:, block, P * f : P * (f + 1)],
+            }
+
         def multiply(c):
             b, chunk_in_graph = divmod(c, CHUNKS_PER_GRAPH)
             codes, planes = code_tiles[c]
             row_cols = slice(chunk_in_graph * P, (chunk_in_graph + 1) * P)
-            accs = []
-            for t in range(TILES):
-                cols = slice(t * P, (t + 1) * P)
-                operands = (
-                    (ROW_BLOCK, row_codes[:, b, row_cols], row_planes[:, b, row_cols]),
-                    (COL_BLOCK, col_codes[:, b, cols], col_planes[:, b, cols]),
-                    (EDGE_BLOCK, codes[:, cols], planes[:, cols]),
+            by_features = stage.tile([P, FEATURE_BLOCKS, TILES * P], F32)
+            for f in range(FEATURE_BLOCKS):
+                acc = psum_features.tile([P, TILES * P], F32)
+                nc.tensor.matmul_mx(
+                    out=acc[:],
+                    rhs=codes[:].bitcast(FP8X4),
+                    rhs_scale=planes[:],
+                    start=True,
+                    stop=False,
+                    **weight(EDGE_BLOCK, f),
                 )
-                acc = psum_acc.tile([P, FEAT], F32, tag="acc")
-                for block, lhs_codes, lhs_planes in operands:
+                nc.tensor.matmul_mx(
+                    out=acc[:],
+                    rhs=col_codes[:, b, :].bitcast(FP8X4),
+                    rhs_scale=col_planes[:, b, :],
+                    start=False,
+                    stop=False,
+                    **weight(COL_BLOCK, f),
+                )
+                for t in range(TILES):
                     nc.tensor.matmul_mx(
-                        out=acc[:],
-                        lhsT=lhs_codes.bitcast(FP8X4),
-                        lhsT_scale=lhs_planes,
-                        rhs=w_words[:, block, :].bitcast(FP4X4),
-                        rhs_scale=w_planes[:, block, :],
-                        start=(block == ROW_BLOCK),
-                        stop=(block == EDGE_BLOCK),
+                        out=acc[:, t * P : (t + 1) * P],
+                        rhs=row_codes[:, b, row_cols].bitcast(FP8X4),
+                        rhs_scale=row_planes[:, b, row_cols],
+                        start=False,
+                        stop=(t == TILES - 1),
+                        **weight(ROW_BLOCK, f),
                     )
-                accs.append(acc)
-            acc_tiles[c] = accs
+                nc.scalar.activation(
+                    out=by_features[:, f, :],
+                    in_=acc[:],
+                    func=ACT.Identity,
+                    bias=bias_column[:, f : f + 1],
+                )
+            edges = []
+            for t in range(TILES):
+                by_rows = psum_rows.tile([P, FEAT], F32)
+                for f in range(FEATURE_BLOCKS):
+                    nc.tensor.transpose(
+                        out=by_rows[:, f * P : (f + 1) * P],
+                        in_=by_features[:, f, t * P : (t + 1) * P],
+                        identity=identity[:],
+                    )
+                edges.append(by_rows)
+            edge_tiles[c] = edges
 
         def add_residual(c):
-            y = y_pool.tile([P, TILES, FEAT], F32)
+            y = row_pool.tile([P, TILES, FEAT], F32)
             sums = stats.tile([P, TILES], F32)
             for t in range(TILES):
                 nc.vector.scalar_tensor_tensor(
                     out=y[:, t, :],
                     in0=emb_tiles[c][:, t, :],
                     scalar=e_mask[:, c, t : t + 1],
-                    in1=acc_tiles[c][t][:],
+                    in1=edge_tiles[c][t][:],
                     op0=ALU.mult,
                     op1=ALU.add,
                     accum_out=sums[:, t : t + 1],
                 )
-            y_tiles[c] = y
-            sum_tiles[c] = sums
+            y_tiles[c] = (y, sums)
 
-        def centre(c):
-            y = y_tiles[c]
+        def mean(c):
             minus_mean = stats.tile([P, TILES], F32)
-            nc.vector.tensor_scalar(
-                out=minus_mean[:],
-                in0=sum_tiles[c][:],
-                scalar1=bias_sum[:, 0:1],
-                scalar2=-1.0 / FEAT,
-                op0=ALU.add,
-                op1=ALU.mult,
-            )
+            nc.vector.tensor_scalar_mul(out=minus_mean[:], in0=y_tiles[c][1][:], scalar1=-1.0 / FEAT)
+            minus_mean_tiles[c] = minus_mean
+
+        def centre_and_gain(c):
+            scaled = row_pool.tile([P, TILES, FEAT], F32)
             for t in range(TILES):
                 nc.vector.scalar_tensor_tensor(
-                    out=y[:, t, :],
-                    in0=y[:, t, :],
-                    scalar=minus_mean[:, t : t + 1],
-                    in1=bias_all[:],
+                    out=scaled[:, t, :],
+                    in0=y_tiles[c][0][:, t, :],
+                    scalar=minus_mean_tiles[c][:, t : t + 1],
+                    in1=gamma_all[:],
                     op0=ALU.add,
-                    op1=ALU.add,
+                    op1=ALU.mult,
                 )
+            scaled_tiles[c] = scaled
 
         def deviation(c):
-            y = y_tiles[c]
             squares = stats.tile([P, TILES], F32)
             for t in range(TILES):
                 nc.scalar.activation(
                     out=squares_unread[:, t, :],
-                    in_=y[:, t, :],
+                    in_=y_tiles[c][0][:, t, :],
                     func=ACT.Square,
+                    bias=minus_mean_tiles[c][:, t : t + 1],
                     accum_out=squares[:, t : t + 1],
                 )
             std = stats.tile([P, TILES], F32)
@@ -321,49 +364,51 @@ def tile_densegatlayer_pb_kernel(
             )
             std_tiles[c] = std
 
-        def normalise(c):
-            y = y_tiles[c]
+        def invert_deviation(c):
             rstd = stats.tile([P, TILES], F32)
             nc.vector.reciprocal(out=rstd[:], in_=std_tiles[c][:])
+            rstd_tiles[c] = rstd
+
+        def normalise_and_store(c):
+            scaled = scaled_tiles[c]
             for t in range(TILES):
                 nc.vector.scalar_tensor_tensor(
-                    out=y[:, t, :],
-                    in0=y[:, t, :],
-                    scalar=rstd[:, t : t + 1],
-                    in1=gamma_all[:],
+                    out=scaled[:, t, :],
+                    in0=scaled[:, t, :],
+                    scalar=rstd_tiles[c][:, t : t + 1],
+                    in1=beta_all[:],
                     op0=ALU.mult,
-                    op1=ALU.mult,
+                    op1=ALU.add,
                 )
-
-        def shift_and_store(c):
-            y = y_tiles[c]
-            nc.vector.tensor_tensor(
-                out=y[:],
-                in0=y[:],
-                in1=beta_all[:].unsqueeze(1).to_broadcast([P, TILES, FEAT]),
-                op=ALU.add,
-            )
-            nc.sync.dma_start(out=out_chunks[c], in_=y[:])
+            nc.sync.dma_start(out=out_chunks[c], in_=scaled[:])
 
         def live(c):
             return 0 <= c < CHUNKS
 
-        for step in range(-2, CHUNKS + 3):
-            if live(step + 2):
-                load(step + 2)
+        for step in range(-3, CHUNKS + 2):
+            if live(step + 3):
+                load(step + 3)
             if live(step + 1):
                 if (step + 1) % CHUNKS_PER_GRAPH == 0:
                     build_node_operands((step + 1) // CHUNKS_PER_GRAPH)
-                mask_and_transpose(step + 1)
+                transpose(step + 1)
             if live(step - 1):
                 add_residual(step - 1)
-                centre(step - 1)
-                deviation(step - 1)
+            if live(step - 2):
+                deviation(step - 2)
             if live(step + 1):
                 regroup(step + 1)
             if live(step):
                 quantise(step)
-                multiply(step)
+            if live(step - 1):
+                mean(step - 1)
             if live(step - 2):
-                normalise(step - 2)
-                shift_and_store(step - 2)
+                invert_deviation(step - 2)
+            if live(step):
+                multiply(step)
+            if live(step - 1):
+                centre_and_gain(step - 1)
+            if live(step - 2):
+                normalise_and_store(step - 2)
+            if live(step + 2):
+                mask(step + 2)

@@ -43,8 +43,9 @@ def tile_densegatlayer_pb_kernel(
     with (
         tc.manual_schedule(),
         tc.tile_pool(name="const", bufs=1) as const,
-        tc.tile_pool(name="emb", bufs=5) as emb_pool,
+        tc.tile_pool(name="emb", bufs=6) as emb_pool,
         tc.tile_pool(name="stage", bufs=2) as stage,
+        tc.tile_pool(name="features", bufs=3) as feature_pool,
         tc.tile_pool(name="rows", bufs=3) as row_pool,
         tc.tile_pool(name="stats", bufs=4) as stats,
         tc.psum_pool(name="psum_xt", bufs=2) as psum_xt,
@@ -208,8 +209,8 @@ def tile_densegatlayer_pb_kernel(
                 out=col_codes[:, b, :].bitcast(FP8X4), scales=col_planes[:, b, :], in_=col_in[:]
             )
 
-        xe_tiles, xt_tiles, grouped_tiles, code_tiles, edge_tiles = {}, {}, {}, {}, {}
-        y_tiles, minus_mean_tiles, std_tiles, rstd_tiles, scaled_tiles = {}, {}, {}, {}, {}
+        xe_tiles, xt_tiles, grouped_tiles, code_tiles, feature_tiles, edge_tiles = {}, {}, {}, {}, {}, {}
+        y_tiles, minus_mean_tiles, square_tiles, rstd_tiles, scaled_tiles = {}, {}, {}, {}, {}
         squares_unread = const.tile([P, TILES, FEAT], BF16)
 
         def mask(c):
@@ -258,6 +259,8 @@ def tile_densegatlayer_pb_kernel(
                 out=codes[:].bitcast(FP8X4), scales=planes[:], in_=grouped_tiles[c][:]
             )
             code_tiles[c] = (codes, planes)
+            by_features = feature_pool.tile([P, FEATURE_BLOCKS, TILES * P], F32)
+            feature_tiles[c] = by_features
 
         def weight(block, f):
             return {
@@ -265,51 +268,51 @@ def tile_densegatlayer_pb_kernel(
                 "lhsT_scale": w_planes[:, block, P * f : P * (f + 1)],
             }
 
-        def multiply(c):
+        def multiply_block(c, f):
             b, chunk_in_graph = divmod(c, CHUNKS_PER_GRAPH)
             codes, planes = code_tiles[c]
             row_cols = slice(chunk_in_graph * P, (chunk_in_graph + 1) * P)
-            by_features = stage.tile([P, FEATURE_BLOCKS, TILES * P], F32)
-            for f in range(FEATURE_BLOCKS):
-                acc = psum_features.tile([P, TILES * P], F32)
+            acc = psum_features.tile([P, TILES * P], F32)
+            nc.tensor.matmul_mx(
+                out=acc[:],
+                rhs=codes[:].bitcast(FP8X4),
+                rhs_scale=planes[:],
+                start=True,
+                stop=False,
+                **weight(EDGE_BLOCK, f),
+            )
+            nc.tensor.matmul_mx(
+                out=acc[:],
+                rhs=col_codes[:, b, :].bitcast(FP8X4),
+                rhs_scale=col_planes[:, b, :],
+                start=False,
+                stop=False,
+                **weight(COL_BLOCK, f),
+            )
+            for t in range(TILES):
                 nc.tensor.matmul_mx(
-                    out=acc[:],
-                    rhs=codes[:].bitcast(FP8X4),
-                    rhs_scale=planes[:],
-                    start=True,
-                    stop=False,
-                    **weight(EDGE_BLOCK, f),
-                )
-                nc.tensor.matmul_mx(
-                    out=acc[:],
-                    rhs=col_codes[:, b, :].bitcast(FP8X4),
-                    rhs_scale=col_planes[:, b, :],
+                    out=acc[:, t * P : (t + 1) * P],
+                    rhs=row_codes[:, b, row_cols].bitcast(FP8X4),
+                    rhs_scale=row_planes[:, b, row_cols],
                     start=False,
-                    stop=False,
-                    **weight(COL_BLOCK, f),
+                    stop=(t == TILES - 1),
+                    **weight(ROW_BLOCK, f),
                 )
-                for t in range(TILES):
-                    nc.tensor.matmul_mx(
-                        out=acc[:, t * P : (t + 1) * P],
-                        rhs=row_codes[:, b, row_cols].bitcast(FP8X4),
-                        rhs_scale=row_planes[:, b, row_cols],
-                        start=False,
-                        stop=(t == TILES - 1),
-                        **weight(ROW_BLOCK, f),
-                    )
-                nc.scalar.activation(
-                    out=by_features[:, f, :],
-                    in_=acc[:],
-                    func=ACT.Identity,
-                    bias=bias_column[:, f : f + 1],
-                )
+            nc.scalar.activation(
+                out=feature_tiles[c][:, f, :],
+                in_=acc[:],
+                func=ACT.Identity,
+                bias=bias_column[:, f : f + 1],
+            )
+
+        def to_rows(c):
             edges = []
             for t in range(TILES):
                 by_rows = psum_rows.tile([P, FEAT], F32)
                 for f in range(FEATURE_BLOCKS):
                     nc.tensor.transpose(
                         out=by_rows[:, f * P : (f + 1) * P],
-                        in_=by_features[:, f, t * P : (t + 1) * P],
+                        in_=feature_tiles[c][:, f, t * P : (t + 1) * P],
                         identity=identity[:],
                     )
                 edges.append(by_rows)
@@ -334,6 +337,8 @@ def tile_densegatlayer_pb_kernel(
             minus_mean = stats.tile([P, TILES], F32)
             nc.vector.tensor_scalar_mul(out=minus_mean[:], in0=y_tiles[c][1][:], scalar1=-1.0 / FEAT)
             minus_mean_tiles[c] = minus_mean
+            squares = stats.tile([P, TILES], F32)
+            square_tiles[c] = squares
 
         def centre_and_gain(c):
             scaled = row_pool.tile([P, TILES, FEAT], F32)
@@ -348,25 +353,24 @@ def tile_densegatlayer_pb_kernel(
                 )
             scaled_tiles[c] = scaled
 
-        def deviation(c):
-            squares = stats.tile([P, TILES], F32)
-            for t in range(TILES):
-                nc.scalar.activation(
-                    out=squares_unread[:, t, :],
-                    in_=y_tiles[c][0][:, t, :],
-                    func=ACT.Square,
-                    bias=minus_mean_tiles[c][:, t : t + 1],
-                    accum_out=squares[:, t : t + 1],
-                )
-            std = stats.tile([P, TILES], F32)
+        def sum_squares(c, t):
             nc.scalar.activation(
-                out=std[:], in_=squares[:], func=ACT.Sqrt, bias=eps[:, 0:1], scale=1.0 / FEAT
+                out=squares_unread[:, t, :],
+                in_=y_tiles[c][0][:, t, :],
+                func=ACT.Square,
+                bias=minus_mean_tiles[c][:, t : t + 1],
+                accum_out=square_tiles[c][:, t : t + 1],
             )
-            std_tiles[c] = std
 
-        def invert_deviation(c):
+        def inverse_deviation(c):
             rstd = stats.tile([P, TILES], F32)
-            nc.vector.reciprocal(out=rstd[:], in_=std_tiles[c][:])
+            nc.scalar.activation(
+                out=rstd[:],
+                in_=square_tiles[c][:],
+                func=ACT.Abs_reciprocal_sqrt,
+                bias=eps[:, 0:1],
+                scale=1.0 / FEAT,
+            )
             rstd_tiles[c] = rstd
 
         def normalise_and_store(c):
@@ -385,30 +389,32 @@ def tile_densegatlayer_pb_kernel(
         def live(c):
             return 0 <= c < CHUNKS
 
-        for step in range(-3, CHUNKS + 2):
+        for step in range(-3, CHUNKS + 3):
             if live(step + 3):
                 load(step + 3)
             if live(step + 1):
                 if (step + 1) % CHUNKS_PER_GRAPH == 0:
                     build_node_operands((step + 1) // CHUNKS_PER_GRAPH)
                 transpose(step + 1)
-            if live(step - 1):
-                add_residual(step - 1)
             if live(step - 2):
-                deviation(step - 2)
-            if live(step + 1):
-                regroup(step + 1)
+                add_residual(step - 2)
+            if live(step - 1):
+                to_rows(step - 1)
             if live(step):
                 quantise(step)
-            if live(step - 1):
-                mean(step - 1)
             if live(step - 2):
-                invert_deviation(step - 2)
-            if live(step):
-                multiply(step)
-            if live(step - 1):
-                centre_and_gain(step - 1)
-            if live(step - 2):
-                normalise_and_store(step - 2)
+                mean(step - 2)
             if live(step + 2):
                 mask(step + 2)
+            if live(step + 1):
+                regroup(step + 1)
+            for k in range(TILES):
+                if live(step - 2):
+                    sum_squares(step - 2, k)
+                if live(step):
+                    multiply_block(step, k)
+            if live(step - 2):
+                inverse_deviation(step - 2)
+                centre_and_gain(step - 2)
+            if live(step - 3):
+                normalise_and_store(step - 3)

@@ -48,9 +48,10 @@ def tile_densegatlayer_pb_kernel(
         tc.tile_pool(name="features", bufs=3) as feature_pool,
         tc.tile_pool(name="rows", bufs=3) as row_pool,
         tc.tile_pool(name="stats", bufs=4) as stats,
+        tc.psum_pool(name="psum_const", bufs=1) as psum_const,
         tc.psum_pool(name="psum_xt", bufs=2) as psum_xt,
         tc.psum_pool(name="psum_features", bufs=2) as psum_features,
-        tc.psum_pool(name="psum_rows", bufs=4) as psum_rows,
+        tc.psum_pool(name="psum_rows", bufs=3) as psum_rows,
     ):
         w_planes = const.tile([P, 3, FEAT], U8, align_bytes=64)
         nc.vector.memset(w_planes[:].bitcast(I32), 0)
@@ -112,8 +113,13 @@ def tile_densegatlayer_pb_kernel(
 
         mask_all = spread(MASK)
         bias_all = spread(BIAS)
-        gamma_psum = spread(GAMMA)
-        beta_psum = spread(BETA)
+        gain_shift = psum_const.tile([P, 2, FEAT], BF16)
+        for slot, which in enumerate((GAMMA, BETA)):
+            nc.tensor.matmul(
+                out=gain_shift[:, slot, :], lhsT=ones[:], rhs=vectors[:, which, :], start=True, stop=True
+            )
+        gamma_all = gain_shift[:, 0, :]
+        beta_all = gain_shift[:, 1, :]
 
         is_i = const.tile([P, I_PER_CHUNK], F32)
         nc.vector.tensor_reduce(
@@ -171,10 +177,6 @@ def tile_densegatlayer_pb_kernel(
         )
         bias_column = const.tile([P, FEATURE_BLOCKS], F32)
         nc.vector.tensor_reduce(out=bias_column[:], in_=picked_bias[:], axis=AXIS_X, op=ALU.add)
-        gamma_all = const.tile([P, FEAT], F32)
-        nc.vector.tensor_copy(out=gamma_all[:], in_=gamma_psum[:])
-        beta_all = const.tile([P, FEAT], F32)
-        nc.vector.tensor_copy(out=beta_all[:], in_=beta_psum[:])
 
         row_codes = const.tile([P, GRAPHS, CHUNKS_PER_GRAPH * P], U32, align_bytes=64)
         row_planes = const.tile([P, GRAPHS, CHUNKS_PER_GRAPH * P], U8, align_bytes=64)
@@ -215,42 +217,39 @@ def tile_densegatlayer_pb_kernel(
 
         def mask(c):
             xe = stage.tile([P, TILES, FEAT], BF16)
-            for t in range(0, TILES, 2):
-                nc.scalar.activation(
-                    out=xe[:, t, :],
-                    in_=emb_tiles[c][:, t, :],
-                    func=ACT.Copy,
-                    scale=e_mask[:, c, t : t + 1],
-                )
-            for t in range(1, TILES, 2):
-                nc.vector.tensor_scalar_mul(
-                    out=xe[:, t, :], in0=emb_tiles[c][:, t, :], scalar1=e_mask[:, c, t : t + 1]
+            for t in range(TILES):
+                nc.gpsimd.tensor_scalar(
+                    out=xe[:, t, :].rearrange("p (u w e) -> p u w e", u=2, e=2),
+                    in0=emb_tiles[c][:, t, :].rearrange("p (w u e) -> p u w e", u=2, e=2),
+                    scalar1=e_mask[:, c, t : t + 1],
+                    scalar2=1.0,
+                    op0=ALU.mult,
+                    op1=ALU.mult,
                 )
             xe_tiles[c] = xe
 
-        def transpose(c):
-            banks = []
-            for half in range(2):
-                xt = psum_xt.tile([P, 2, 2, P], F32, tag="xt")
-                for a in range(2):
-                    for u in range(2):
-                        nc.tensor.transpose(
-                            out=xt[:, a, u, :],
-                            in_=xe_tiles[c][:, 2 * half + a, :].bitcast(F32)[:, u:WORDS:2],
-                            identity=identity[:],
-                        )
-                banks.append(xt)
-            xt_tiles[c] = banks
+        def transpose(c, half):
+            xt = psum_xt.tile([P, 2, 2, P], F32, tag="xt")
+            for a in range(2):
+                for u in range(2):
+                    nc.tensor.transpose(
+                        out=xt[:, a, u, :],
+                        in_=xe_tiles[c][:, 2 * half + a, :].bitcast(F32)[:, u * P : (u + 1) * P],
+                        identity=identity[:],
+                    )
+            xt_tiles[c, half] = xt
 
-        def regroup(c):
-            grouped = stage.tile([P, TILES * P * PACK], BF16, align_bytes=64)
-            grouped_words = grouped[:].bitcast(F32).rearrange("p (t r u) -> p t r u", t=TILES, u=2)
-            for half in range(2):
-                nc.scalar.copy(
-                    out=grouped_words[:, 2 * half : 2 * half + 2],
-                    in_=xt_tiles[c][half][:].rearrange("p a u r -> p a r u"),
-                )
-            grouped_tiles[c] = grouped
+        def regroup(c, half):
+            if half == 0:
+                grouped = stage.tile([P, TILES * P * PACK], BF16, align_bytes=64)
+                grouped_tiles[c] = grouped
+            grouped_words = (
+                grouped_tiles[c][:].bitcast(F32).rearrange("p (t r u) -> p t r u", t=TILES, u=2)
+            )
+            nc.scalar.copy(
+                out=grouped_words[:, 2 * half : 2 * half + 2],
+                in_=xt_tiles[c, half][:].rearrange("p a u r -> p a r u"),
+            )
 
         def quantise(c):
             codes = stage.tile([P, TILES * P], U32, align_bytes=64)
@@ -305,37 +304,37 @@ def tile_densegatlayer_pb_kernel(
                 bias=bias_column[:, f : f + 1],
             )
 
-        def to_rows(c):
-            edges = []
-            for t in range(TILES):
-                by_rows = psum_rows.tile([P, FEAT], F32)
-                for f in range(FEATURE_BLOCKS):
-                    nc.tensor.transpose(
-                        out=by_rows[:, f * P : (f + 1) * P],
-                        in_=feature_tiles[c][:, f, t * P : (t + 1) * P],
-                        identity=identity[:],
-                    )
-                edges.append(by_rows)
-            edge_tiles[c] = edges
-
-        def add_residual(c):
-            y = row_pool.tile([P, TILES, FEAT], F32)
-            sums = stats.tile([P, TILES], F32)
-            for t in range(TILES):
-                nc.vector.scalar_tensor_tensor(
-                    out=y[:, t, :],
-                    in0=emb_tiles[c][:, t, :],
-                    scalar=e_mask[:, c, t : t + 1],
-                    in1=edge_tiles[c][t][:],
-                    op0=ALU.mult,
-                    op1=ALU.add,
-                    accum_out=sums[:, t : t + 1],
+        def to_rows(c, t):
+            by_rows = psum_rows.tile([P, FEAT], F32)
+            for f in range(FEATURE_BLOCKS):
+                nc.tensor.transpose(
+                    out=by_rows[:, f * P : (f + 1) * P],
+                    in_=feature_tiles[c][:, f, t * P : (t + 1) * P],
+                    identity=identity[:],
                 )
-            y_tiles[c] = (y, sums)
+            edge_tiles[c, t] = by_rows
+
+        def add_residual(c, t):
+            if t == 0:
+                y = row_pool.tile([P, TILES, FEAT], F32)
+                sums = stats.tile([P, TILES], F32)
+                y_tiles[c] = (y, sums)
+            y, sums = y_tiles[c]
+            nc.vector.scalar_tensor_tensor(
+                out=y[:, t, :],
+                in0=emb_tiles[c][:, t, :],
+                scalar=e_mask[:, c, t : t + 1],
+                in1=edge_tiles[c, t][:],
+                op0=ALU.mult,
+                op1=ALU.add,
+                accum_out=sums[:, t : t + 1],
+            )
 
         def mean(c):
             minus_mean = stats.tile([P, TILES], F32)
-            nc.vector.tensor_scalar_mul(out=minus_mean[:], in0=y_tiles[c][1][:], scalar1=-1.0 / FEAT)
+            nc.scalar.activation(
+                out=minus_mean[:], in_=y_tiles[c][1][:], func=ACT.Copy, scale=-1.0 / FEAT
+            )
             minus_mean_tiles[c] = minus_mean
             squares = stats.tile([P, TILES], F32)
             square_tiles[c] = squares
@@ -347,7 +346,7 @@ def tile_densegatlayer_pb_kernel(
                     out=scaled[:, t, :],
                     in0=y_tiles[c][0][:, t, :],
                     scalar=minus_mean_tiles[c][:, t : t + 1],
-                    in1=gamma_all[:],
+                    in1=gamma_all,
                     op0=ALU.add,
                     op1=ALU.mult,
                 )
@@ -380,7 +379,7 @@ def tile_densegatlayer_pb_kernel(
                     out=scaled[:, t, :],
                     in0=scaled[:, t, :],
                     scalar=rstd_tiles[c][:, t : t + 1],
-                    in1=beta_all[:],
+                    in1=beta_all,
                     op0=ALU.mult,
                     op1=ALU.add,
                 )
@@ -392,22 +391,26 @@ def tile_densegatlayer_pb_kernel(
         for step in range(-3, CHUNKS + 3):
             if live(step + 3):
                 load(step + 3)
-            if live(step + 1):
-                if (step + 1) % CHUNKS_PER_GRAPH == 0:
-                    build_node_operands((step + 1) // CHUNKS_PER_GRAPH)
-                transpose(step + 1)
-            if live(step - 2):
-                add_residual(step - 2)
-            if live(step - 1):
-                to_rows(step - 1)
+            if live(step + 1) and (step + 1) % CHUNKS_PER_GRAPH == 0:
+                build_node_operands((step + 1) // CHUNKS_PER_GRAPH)
             if live(step):
                 quantise(step)
+            if live(step + 1):
+                transpose(step + 1, 0)
+                transpose(step + 1, 1)
+                regroup(step + 1, 0)
+                regroup(step + 1, 1)
+            for t in range(TILES):
+                if live(step - 2):
+                    add_residual(step - 2, t)
+                if t == 0 and live(step - 2):
+                    to_rows(step - 2, TILES - 1)
+                if t > 0 and live(step - 1):
+                    to_rows(step - 1, t - 1)
             if live(step - 2):
                 mean(step - 2)
             if live(step + 2):
                 mask(step + 2)
-            if live(step + 1):
-                regroup(step + 1)
             for k in range(TILES):
                 if live(step - 2):
                     sum_squares(step - 2, k)
@@ -415,6 +418,7 @@ def tile_densegatlayer_pb_kernel(
                     multiply_block(step, k)
             if live(step - 2):
                 inverse_deviation(step - 2)
-                centre_and_gain(step - 2)
             if live(step - 3):
                 normalise_and_store(step - 3)
+            if live(step - 2):
+                centre_and_gain(step - 2)

@@ -27,6 +27,10 @@ CHUNKS_PER_GRAPH = CHUNKS // GRAPHS
 I_PER_CHUNK = CHUNK_ROWS // NODES
 J_GROUPS = NODES // TILES
 
+PAIR = 2
+PAIRS = 2 * CHUNKS
+GPSIMD_TILES = ()
+
 FEATURE_BLOCKS = FEAT // P
 ROW_BLOCK, COL_BLOCK, EDGE_BLOCK = 0, 1, 2
 
@@ -43,15 +47,16 @@ def tile_densegatlayer_pb_kernel(
     with (
         tc.manual_schedule(),
         tc.tile_pool(name="const", bufs=1) as const,
-        tc.tile_pool(name="emb", bufs=6) as emb_pool,
+        tc.tile_pool(name="emb", bufs=7) as emb_pool,
+        tc.tile_pool(name="xe", bufs=4) as xe_pool,
         tc.tile_pool(name="stage", bufs=2) as stage,
         tc.tile_pool(name="features", bufs=3) as feature_pool,
-        tc.tile_pool(name="rows", bufs=3) as row_pool,
-        tc.tile_pool(name="stats", bufs=4) as stats,
+        tc.tile_pool(name="rows", bufs=4) as row_pool,
+        tc.tile_pool(name="stats", bufs=6) as stats,
         tc.psum_pool(name="psum_const", bufs=1) as psum_const,
-        tc.psum_pool(name="psum_xt", bufs=2) as psum_xt,
+        tc.psum_pool(name="psum_xt", bufs=1) as psum_xt,
         tc.psum_pool(name="psum_features", bufs=2) as psum_features,
-        tc.psum_pool(name="psum_rows", bufs=3) as psum_rows,
+        tc.psum_pool(name="psum_rows", bufs=4) as psum_rows,
     ):
         w_planes = const.tile([P, 3, FEAT], U8, align_bytes=64)
         nc.vector.memset(w_planes[:].bitcast(I32), 0)
@@ -67,6 +72,7 @@ def tile_densegatlayer_pb_kernel(
             nc.sync.dma_start(out=emb[:], in_=emb_chunks[c])
             emb_tiles[c] = emb
 
+        load(0)
         scales_i32 = Wedge_scales.bitcast(I32)
         for quadrant in range(4):
             nc.sync.dma_start(
@@ -120,6 +126,8 @@ def tile_densegatlayer_pb_kernel(
             )
         gamma_all = gain_shift[:, 0, :]
         beta_all = gain_shift[:, 1, :]
+        gain_shift_sbuf = const.tile([P, 2, FEAT], F32)
+        nc.vector.tensor_copy(out=gain_shift_sbuf[:], in_=gain_shift[:])
 
         is_i = const.tile([P, I_PER_CHUNK], F32)
         nc.vector.tensor_reduce(
@@ -183,63 +191,84 @@ def tile_densegatlayer_pb_kernel(
         col_codes = const.tile([P, GRAPHS, TILES * P], U32, align_bytes=64)
         col_planes = const.tile([P, GRAPHS, TILES * P], U8, align_bytes=64)
 
-        def build_node_operands(b):
-            nodes = node_words[:, :, b * NODES : (b + 1) * NODES]
-            row_in = stage.tile([P, NODES * J_GROUPS * PACK], BF16, align_bytes=64)
-            nc.scalar.copy(
-                out=row_in[:].bitcast(F32).rearrange("p (n g u) -> p n g u", g=J_GROUPS, u=2),
-                in_=nodes.rearrange("p u n -> p n u")
+        node_inputs = {}
+        NODES_PER_PIECE = NODES // TILES
+
+        def copy_row_nodes(b, piece, copy):
+            if piece == 0:
+                row_in = stage.tile([P, NODES * J_GROUPS * PACK], BF16, align_bytes=64)
+                col_in = stage.tile([P, TILES * P * PACK], BF16, align_bytes=64)
+                node_inputs[b] = (row_in, col_in)
+            first = piece * NODES_PER_PIECE
+            copy(
+                out=node_inputs[b][0][:]
+                .bitcast(F32)
+                .rearrange("p (n g u) -> p n g u", g=J_GROUPS, u=2)[:, first : first + NODES_PER_PIECE],
+                in_=node_words[:, :, b * NODES + first : b * NODES + first + NODES_PER_PIECE]
+                .rearrange("p u n -> p n u")
                 .unsqueeze(2)
-                .to_broadcast([P, NODES, J_GROUPS, 2]),
+                .to_broadcast([P, NODES_PER_PIECE, J_GROUPS, 2]),
             )
-            col_in = stage.tile([P, TILES * P * PACK], BF16, align_bytes=64)
-            col_in_words = col_in[:].bitcast(F32).rearrange(
-                "p (t a g u) -> p t a g u", t=TILES, a=I_PER_CHUNK, u=2
+
+        def copy_col_nodes(b, t, copy):
+            copy(
+                out=node_inputs[b][1][:]
+                .bitcast(F32)
+                .rearrange("p (t a g u) -> p t a g u", t=TILES, a=I_PER_CHUNK, u=2)[:, t],
+                in_=node_words[:, :, b * NODES + t : (b + 1) * NODES : TILES]
+                .rearrange("p u g -> p g u")
+                .unsqueeze(1)
+                .to_broadcast([P, I_PER_CHUNK, J_GROUPS, 2]),
             )
-            for t in range(TILES):
-                nc.scalar.copy(
-                    out=col_in_words[:, t],
-                    in_=nodes[:, :, t:NODES:TILES]
-                    .rearrange("p u g -> p g u")
-                    .unsqueeze(1)
-                    .to_broadcast([P, I_PER_CHUNK, J_GROUPS, 2]),
-                )
-            nc.vector.quantize_mx(
-                out=row_codes[:, b, :].bitcast(FP8X4), scales=row_planes[:, b, :], in_=row_in[:]
-            )
+
+        def quantise_node_operands(b):
+            row_in, col_in = node_inputs[b]
             nc.vector.quantize_mx(
                 out=col_codes[:, b, :].bitcast(FP8X4), scales=col_planes[:, b, :], in_=col_in[:]
+            )
+            nc.vector.quantize_mx(
+                out=row_codes[:, b, :].bitcast(FP8X4), scales=row_planes[:, b, :], in_=row_in[:]
             )
 
         xe_tiles, xt_tiles, grouped_tiles, code_tiles, feature_tiles, edge_tiles = {}, {}, {}, {}, {}, {}
         y_tiles, minus_mean_tiles, square_tiles, rstd_tiles, scaled_tiles = {}, {}, {}, {}, {}
-        squares_unread = const.tile([P, TILES, FEAT], BF16)
+        squares_unread = const.tile([P, FEAT], BF16)
 
-        def mask(c):
-            xe = stage.tile([P, TILES, FEAT], BF16)
-            for t in range(TILES):
-                nc.gpsimd.tensor_scalar(
-                    out=xe[:, t, :].rearrange("p (u w e) -> p u w e", u=2, e=2),
-                    in0=emb_tiles[c][:, t, :].rearrange("p (w u e) -> p u w e", u=2, e=2),
-                    scalar1=e_mask[:, c, t : t + 1],
-                    scalar2=1.0,
-                    op0=ALU.mult,
-                    op1=ALU.mult,
-                )
-            xe_tiles[c] = xe
+        def mask(j, on_vector):
+            c, half = divmod(j, 2)
+            xe = xe_pool.tile([P, PAIR, FEAT], BF16)
+            for a in range(PAIR):
+                t = PAIR * half + a
+                xe_words = xe[:, a, :].rearrange("p (u w e) -> p u w e", u=2, e=2)
+                emb_words = emb_tiles[c][:, t, :].rearrange("p (w u e) -> p u w e", u=2, e=2)
+                if on_vector:
+                    nc.vector.tensor_scalar_mul(
+                        out=xe_words, in0=emb_words, scalar1=e_mask[:, c, t : t + 1]
+                    )
+                else:
+                    nc.gpsimd.tensor_scalar(
+                        out=xe_words,
+                        in0=emb_words,
+                        scalar1=e_mask[:, c, t : t + 1],
+                        scalar2=1.0,
+                        op0=ALU.mult,
+                        op1=ALU.mult,
+                    )
+            xe_tiles[j] = xe
 
-        def transpose(c, half):
-            xt = psum_xt.tile([P, 2, 2, P], F32, tag="xt")
-            for a in range(2):
+        def transpose(j):
+            xt = psum_xt.tile([P, PAIR, 2, P], F32, tag="xt")
+            for a in range(PAIR):
                 for u in range(2):
                     nc.tensor.transpose(
                         out=xt[:, a, u, :],
-                        in_=xe_tiles[c][:, 2 * half + a, :].bitcast(F32)[:, u * P : (u + 1) * P],
+                        in_=xe_tiles[j][:, a, :].bitcast(F32)[:, u * P : (u + 1) * P],
                         identity=identity[:],
                     )
-            xt_tiles[c, half] = xt
+            xt_tiles[j] = xt
 
-        def regroup(c, half):
+        def regroup(j):
+            c, half = divmod(j, 2)
             if half == 0:
                 grouped = stage.tile([P, TILES * P * PACK], BF16, align_bytes=64)
                 grouped_tiles[c] = grouped
@@ -247,8 +276,8 @@ def tile_densegatlayer_pb_kernel(
                 grouped_tiles[c][:].bitcast(F32).rearrange("p (t r u) -> p t r u", t=TILES, u=2)
             )
             nc.scalar.copy(
-                out=grouped_words[:, 2 * half : 2 * half + 2],
-                in_=xt_tiles[c, half][:].rearrange("p a u r -> p a r u"),
+                out=grouped_words[:, PAIR * half : PAIR * half + PAIR],
+                in_=xt_tiles[j][:].rearrange("p a u r -> p a r u"),
             )
 
         def quantise(c):
@@ -266,6 +295,8 @@ def tile_densegatlayer_pb_kernel(
                 "lhsT": w_words[:, block, 2 * P * f : 2 * P * (f + 1)].bitcast(FP4X4),
                 "lhsT_scale": w_planes[:, block, P * f : P * (f + 1)],
             }
+
+        acc_tiles = {}
 
         def multiply_block(c, f):
             b, chunk_in_graph = divmod(c, CHUNKS_PER_GRAPH)
@@ -297,128 +328,185 @@ def tile_densegatlayer_pb_kernel(
                     stop=(t == TILES - 1),
                     **weight(ROW_BLOCK, f),
                 )
+            acc_tiles[c, f] = acc
+
+        def copy_block(c, f):
             nc.scalar.activation(
                 out=feature_tiles[c][:, f, :],
-                in_=acc[:],
+                in_=acc_tiles[c, f][:],
                 func=ACT.Identity,
                 bias=bias_column[:, f : f + 1],
             )
 
-        def to_rows(c, t):
-            by_rows = psum_rows.tile([P, FEAT], F32)
-            for f in range(FEATURE_BLOCKS):
-                nc.tensor.transpose(
-                    out=by_rows[:, f * P : (f + 1) * P],
-                    in_=feature_tiles[c][:, f, t * P : (t + 1) * P],
-                    identity=identity[:],
-                )
-            edge_tiles[c, t] = by_rows
+        def to_rows(j):
+            c, half = divmod(j, 2)
+            for a in range(PAIR):
+                t = PAIR * half + a
+                by_rows = psum_rows.tile([P, FEAT], F32)
+                for f in range(FEATURE_BLOCKS):
+                    nc.tensor.transpose(
+                        out=by_rows[:, f * P : (f + 1) * P],
+                        in_=feature_tiles[c][:, f, t * P : (t + 1) * P],
+                        identity=identity[:],
+                    )
+                edge_tiles[j, a] = by_rows
 
-        def add_residual(c, t):
-            if t == 0:
-                y = row_pool.tile([P, TILES, FEAT], F32)
-                sums = stats.tile([P, TILES], F32)
-                y_tiles[c] = (y, sums)
-            y, sums = y_tiles[c]
-            nc.vector.scalar_tensor_tensor(
-                out=y[:, t, :],
-                in0=emb_tiles[c][:, t, :],
-                scalar=e_mask[:, c, t : t + 1],
-                in1=edge_tiles[c, t][:],
-                op0=ALU.mult,
-                op1=ALU.add,
-                accum_out=sums[:, t : t + 1],
-            )
-
-        def mean(c):
-            minus_mean = stats.tile([P, TILES], F32)
-            nc.scalar.activation(
-                out=minus_mean[:], in_=y_tiles[c][1][:], func=ACT.Copy, scale=-1.0 / FEAT
-            )
-            minus_mean_tiles[c] = minus_mean
-            squares = stats.tile([P, TILES], F32)
-            square_tiles[c] = squares
-
-        def centre_and_gain(c):
-            scaled = row_pool.tile([P, TILES, FEAT], F32)
-            for t in range(TILES):
+        def add_residual(j):
+            c, half = divmod(j, 2)
+            y = row_pool.tile([P, PAIR, FEAT], F32)
+            sums = stats.tile([P, PAIR], F32)
+            for a in range(PAIR):
+                t = PAIR * half + a
                 nc.vector.scalar_tensor_tensor(
-                    out=scaled[:, t, :],
-                    in0=y_tiles[c][0][:, t, :],
-                    scalar=minus_mean_tiles[c][:, t : t + 1],
-                    in1=gamma_all,
-                    op0=ALU.add,
-                    op1=ALU.mult,
+                    out=y[:, a, :],
+                    in0=emb_tiles[c][:, t, :],
+                    scalar=e_mask[:, c, t : t + 1],
+                    in1=edge_tiles[j, a][:],
+                    op0=ALU.mult,
+                    op1=ALU.add,
+                    accum_out=sums[:, a : a + 1],
                 )
-            scaled_tiles[c] = scaled
+            y_tiles[j] = (y, sums)
 
-        def sum_squares(c, t):
+        def mean(j):
+            minus_mean = stats.tile([P, PAIR], F32)
             nc.scalar.activation(
-                out=squares_unread[:, t, :],
-                in_=y_tiles[c][0][:, t, :],
+                out=minus_mean[:], in_=y_tiles[j][1][:], func=ACT.Copy, scale=-1.0 / FEAT
+            )
+            minus_mean_tiles[j] = minus_mean
+            squares = stats.tile([P, PAIR], F32)
+            square_tiles[j] = squares
+
+        def on_gpsimd(j, a):
+            return PAIR * (j % 2) + a in GPSIMD_TILES
+
+        def centre_and_gain(j):
+            scaled = row_pool.tile([P, PAIR, FEAT], F32)
+            for a in range(PAIR):
+                if not on_gpsimd(j, a):
+                    nc.vector.scalar_tensor_tensor(
+                        out=scaled[:, a, :],
+                        in0=y_tiles[j][0][:, a, :],
+                        scalar=minus_mean_tiles[j][:, a : a + 1],
+                        in1=gamma_all,
+                        op0=ALU.add,
+                        op1=ALU.mult,
+                    )
+            scaled_tiles[j] = scaled
+
+        def sum_squares(j, a):
+            nc.scalar.activation(
+                out=squares_unread[:],
+                in_=y_tiles[j][0][:, a, :],
                 func=ACT.Square,
-                bias=minus_mean_tiles[c][:, t : t + 1],
-                accum_out=square_tiles[c][:, t : t + 1],
+                bias=minus_mean_tiles[j][:, a : a + 1],
+                accum_out=square_tiles[j][:, a : a + 1],
             )
 
-        def inverse_deviation(c):
-            rstd = stats.tile([P, TILES], F32)
+        def inverse_deviation(j):
+            rstd = stats.tile([P, PAIR], F32)
             nc.scalar.activation(
                 out=rstd[:],
-                in_=square_tiles[c][:],
+                in_=square_tiles[j][:],
                 func=ACT.Abs_reciprocal_sqrt,
                 bias=eps[:, 0:1],
                 scale=1.0 / FEAT,
             )
-            rstd_tiles[c] = rstd
+            rstd_tiles[j] = rstd
 
-        def normalise_and_store(c):
-            scaled = scaled_tiles[c]
-            for t in range(TILES):
-                nc.vector.scalar_tensor_tensor(
-                    out=scaled[:, t, :],
-                    in0=scaled[:, t, :],
-                    scalar=rstd_tiles[c][:, t : t + 1],
-                    in1=beta_all,
-                    op0=ALU.mult,
-                    op1=ALU.add,
-                )
-            nc.sync.dma_start(out=out_chunks[c], in_=scaled[:])
+        def normalise_on_gpsimd(j):
+            scaled = scaled_tiles[j]
+            for a in range(PAIR):
+                if on_gpsimd(j, a):
+                    nc.gpsimd.tensor_scalar(
+                        out=scaled[:, a, :],
+                        in0=y_tiles[j][0][:, a, :],
+                        scalar1=minus_mean_tiles[j][:, a : a + 1],
+                        scalar2=rstd_tiles[j][:, a : a + 1],
+                        op0=ALU.add,
+                        op1=ALU.mult,
+                    )
+                    nc.gpsimd.tensor_tensor(
+                        out=scaled[:, a, :], in0=scaled[:, a, :], in1=gain_shift_sbuf[:, 0, :], op=ALU.mult
+                    )
+                    nc.gpsimd.tensor_tensor(
+                        out=scaled[:, a, :], in0=scaled[:, a, :], in1=gain_shift_sbuf[:, 1, :], op=ALU.add
+                    )
 
-        def live(c):
-            return 0 <= c < CHUNKS
+        def normalise(j):
+            scaled = scaled_tiles[j]
+            for a in range(PAIR):
+                if not on_gpsimd(j, a):
+                    nc.vector.scalar_tensor_tensor(
+                        out=scaled[:, a, :],
+                        in0=scaled[:, a, :],
+                        scalar=rstd_tiles[j][:, a : a + 1],
+                        in1=beta_all,
+                        op0=ALU.mult,
+                        op1=ALU.add,
+                    )
 
-        for step in range(-3, CHUNKS + 3):
-            if live(step + 3):
-                load(step + 3)
-            if live(step + 1) and (step + 1) % CHUNKS_PER_GRAPH == 0:
-                build_node_operands((step + 1) // CHUNKS_PER_GRAPH)
-            if live(step):
-                quantise(step)
-            if live(step + 1):
-                transpose(step + 1, 0)
-                transpose(step + 1, 1)
-                regroup(step + 1, 0)
-                regroup(step + 1, 1)
-            for t in range(TILES):
-                if live(step - 2):
-                    add_residual(step - 2, t)
-                if t == 0 and live(step - 2):
-                    to_rows(step - 2, TILES - 1)
-                if t > 0 and live(step - 1):
-                    to_rows(step - 1, t - 1)
-            if live(step - 2):
-                mean(step - 2)
-            if live(step + 2):
-                mask(step + 2)
-            for k in range(TILES):
-                if live(step - 2):
-                    sum_squares(step - 2, k)
-                if live(step):
-                    multiply_block(step, k)
-            if live(step - 2):
-                inverse_deviation(step - 2)
-            if live(step - 3):
-                normalise_and_store(step - 3)
-            if live(step - 2):
-                centre_and_gain(step - 2)
+        def store(j):
+            c, half = divmod(j, 2)
+            nc.sync.dma_start(
+                out=out_chunks[c][:, PAIR * half : PAIR * half + PAIR, :], in_=scaled_tiles[j][:]
+            )
+
+        def pair(j):
+            return 0 <= j < PAIRS
+
+        VECTOR_MASKS = 4
+
+        for h in range(-9, PAIRS + 6):
+            if h % 2 != 0 and 1 <= (h + 9) // 2 < CHUNKS:
+                load((h + 9) // 2)
+            if h == -4:
+                for piece in range(TILES):
+                    copy_row_nodes(0, piece, nc.scalar.copy)
+                for t in range(TILES):
+                    copy_col_nodes(0, t, nc.vector.tensor_copy)
+            if pair(h + 5) and h + 5 < VECTOR_MASKS:
+                mask(h + 5, True)
+            if h == -2:
+                quantise_node_operands(0)
+            if pair(h - 3):
+                add_residual(h - 3)
+            if pair(h + 2):
+                regroup(h + 2)
+            first_block = 2 * (h % 2)
+            if pair(h):
+                multiply_block(h // 2, first_block)
+            if pair(h - 4):
+                sum_squares(h - 4, 0)
+            if pair(h):
+                copy_block(h // 2, first_block)
+                multiply_block(h // 2, first_block + 1)
+            if pair(h - 4):
+                sum_squares(h - 4, 1)
+            if pair(h - 3):
+                mean(h - 3)
+            if pair(h):
+                copy_block(h // 2, first_block + 1)
+            if pair(h - 4):
+                inverse_deviation(h - 4)
+            if 4 <= h < 4 + TILES:
+                copy_row_nodes(1, h - 4, nc.scalar.copy)
+            if 4 + TILES <= h < 4 + 2 * TILES:
+                copy_col_nodes(1, h - 4 - TILES, nc.scalar.copy)
+            if h == 4 + 2 * TILES:
+                quantise_node_operands(1)
+            if h % 2 != 0 and pair(h + 1):
+                quantise((h + 1) // 2)
+            if pair(h - 4):
+                centre_and_gain(h - 4)
+            if pair(h - 5):
+                normalise(h - 5)
+            if pair(h - 2):
+                to_rows(h - 2)
+            if pair(h + 3):
+                transpose(h + 3)
+            if pair(h + 5) and h + 5 >= VECTOR_MASKS:
+                mask(h + 5, False)
+            if pair(h - 5):
+                normalise_on_gpsimd(h - 5)
+                store(h - 5)

@@ -29,7 +29,7 @@ J_GROUPS = NODES // TILES
 
 PAIR = 2
 PAIRS = 2 * CHUNKS
-GPSIMD_TILES = ()
+GPSIMD_TILES = (3,)
 
 FEATURE_BLOCKS = FEAT // P
 ROW_BLOCK, COL_BLOCK, EDGE_BLOCK = 0, 1, 2

@@ -221,13 +221,19 @@ def tile_densegatlayer_pb_kernel(
                 .to_broadcast([P, I_PER_CHUNK, J_GROUPS, 2]),
             )
 
-        def quantise_node_operands(b):
-            row_in, col_in = node_inputs[b]
+        def quantise_col_nodes(b):
             nc.vector.quantize_mx(
-                out=col_codes[:, b, :].bitcast(FP8X4), scales=col_planes[:, b, :], in_=col_in[:]
+                out=col_codes[:, b, :].bitcast(FP8X4),
+                scales=col_planes[:, b, :],
+                in_=node_inputs[b][1][:],
             )
+
+        def quantise_row_nodes(b, first, pieces):
+            cols = slice(first * NODES_PER_PIECE * J_GROUPS, (first + pieces) * NODES_PER_PIECE * J_GROUPS)
             nc.vector.quantize_mx(
-                out=row_codes[:, b, :].bitcast(FP8X4), scales=row_planes[:, b, :], in_=row_in[:]
+                out=row_codes[:, b, cols].bitcast(FP8X4),
+                scales=row_planes[:, b, cols],
+                in_=node_inputs[b][0][:, PACK * cols.start : PACK * cols.stop],
             )
 
         xe_tiles, xt_tiles, grouped_tiles, code_tiles, feature_tiles, edge_tiles = {}, {}, {}, {}, {}, {}
@@ -378,6 +384,8 @@ def tile_densegatlayer_pb_kernel(
             square_tiles[j] = squares
 
         def on_gpsimd(j, a):
+            if j // 2 == CHUNKS - 1:
+                return j % 2 == 0 and a == 1
             return PAIR * (j % 2) + a in GPSIMD_TILES
 
         def centre_and_gain(j):
@@ -460,20 +468,23 @@ def tile_densegatlayer_pb_kernel(
         for h in range(-9, PAIRS + 6):
             if h % 2 != 0 and 1 <= (h + 9) // 2 < CHUNKS:
                 load((h + 9) // 2)
-            if h == -4:
-                for piece in range(TILES):
-                    copy_row_nodes(0, piece, nc.scalar.copy)
-                for t in range(TILES):
-                    copy_col_nodes(0, t, nc.vector.tensor_copy)
-            if pair(h + 5) and h + 5 < VECTOR_MASKS:
+            if -5 <= h <= -3:
                 mask(h + 5, True)
+            if h == -4:
+                copy_row_nodes(0, 0, nc.scalar.copy)
+                for t in range(TILES):
+                    copy_col_nodes(0, t, nc.vector.tensor_copy if t < PAIR else nc.scalar.copy)
             if h == -2:
-                quantise_node_operands(0)
+                quantise_row_nodes(0, 0, 1)
+                quantise_col_nodes(0)
             if pair(h - 3):
                 add_residual(h - 3)
             if pair(h + 2):
                 regroup(h + 2)
             first_block = 2 * (h % 2)
+            rows_first = h in (2, 3)
+            if rows_first:
+                to_rows(h - 2)
             if pair(h):
                 multiply_block(h // 2, first_block)
             if pair(h - 4):
@@ -494,14 +505,23 @@ def tile_densegatlayer_pb_kernel(
             if 4 + TILES <= h < 4 + 2 * TILES:
                 copy_col_nodes(1, h - 4 - TILES, nc.scalar.copy)
             if h == 4 + 2 * TILES:
-                quantise_node_operands(1)
+                quantise_col_nodes(1)
+                quantise_row_nodes(1, 0, TILES)
             if h % 2 != 0 and pair(h + 1):
                 quantise((h + 1) // 2)
+            if h == -1:
+                mask(VECTOR_MASKS - 1, True)
+            if -1 <= h <= 1:
+                copy_row_nodes(0, h + 2, nc.scalar.copy)
+            if h == 0:
+                quantise_row_nodes(0, 1, 1)
+            if h == 2:
+                quantise_row_nodes(0, 2, 2)
             if pair(h - 4):
                 centre_and_gain(h - 4)
             if pair(h - 5):
                 normalise(h - 5)
-            if pair(h - 2):
+            if pair(h - 2) and not rows_first:
                 to_rows(h - 2)
             if pair(h + 3):
                 transpose(h + 3)

@@ -47,8 +47,8 @@ def tile_densegatlayer_pb_kernel(
     with (
         tc.manual_schedule(),
         tc.tile_pool(name="const", bufs=1) as const,
-        tc.tile_pool(name="emb", bufs=7) as emb_pool,
-        tc.tile_pool(name="xe", bufs=4) as xe_pool,
+        tc.tile_pool(name="emb", bufs=11) as emb_pool,
+        tc.tile_pool(name="xe", bufs=12) as xe_pool,
         tc.tile_pool(name="stage", bufs=2) as stage,
         tc.tile_pool(name="features", bufs=3) as feature_pool,
         tc.tile_pool(name="rows", bufs=4) as row_pool,
@@ -58,10 +58,10 @@ def tile_densegatlayer_pb_kernel(
         tc.psum_pool(name="psum_features", bufs=2) as psum_features,
         tc.psum_pool(name="psum_rows", bufs=4) as psum_rows,
     ):
-        w_planes = const.tile([P, 3, FEAT], U8, align_bytes=64)
-        nc.vector.memset(w_planes[:].bitcast(I32), 0)
-        w_words = const.tile([P, 3, 2 * FEAT], U8, align_bytes=64)
-
+        mask_all = const.tile([P, GRAPHS * NODES], BF16)
+        nc.scalar.dma_start(
+            out=mask_all[:], in_=node_mask.rearrange("b n -> (b n)").partition_broadcast(P)
+        )
         node_rows = const.tile([P, FEAT], BF16)
         nc.sync.dma_start(out=node_rows[:], in_=new_node.flatten_outer_dims())
 
@@ -73,6 +73,10 @@ def tile_densegatlayer_pb_kernel(
             emb_tiles[c] = emb
 
         load(0)
+
+        w_planes = const.tile([P, 3, FEAT], U8, align_bytes=64)
+        nc.vector.memset(w_planes[:].bitcast(I32), 0)
+        w_words = const.tile([P, 3, 2 * FEAT], U8, align_bytes=64)
         scales_i32 = Wedge_scales.bitcast(I32)
         for quadrant in range(4):
             nc.sync.dma_start(
@@ -83,14 +87,14 @@ def tile_densegatlayer_pb_kernel(
             out=w_words[:].bitcast(I32), in_=Wedge_words.bitcast(I32).rearrange("g p n -> p g n")
         )
 
-        BIAS, GAMMA, BETA, MASK = 0, 1, 2, 3
-        vectors = const.tile([P, 4, FEAT], BF16)
-        nc.vector.memset(vectors[:], 0.0)
+        bias_rows = const.tile([P, P], BF16)
+        nc.vector.memset(bias_rows[:], 0.0)
         nc.scalar.dma_start(
-            out=vectors[0:1, MASK, 0 : GRAPHS * NODES],
-            in_=node_mask.rearrange("(o b) n -> o (b n)", o=1),
+            out=bias_rows[0:FEATURE_BLOCKS, :], in_=bedge.rearrange("(f q) -> f q", q=P)
         )
-        nc.scalar.dma_start(out=vectors[0:1, BIAS, :], in_=bedge.rearrange("(o n) -> o n", o=1))
+        GAMMA, BETA = 0, 1
+        vectors = const.tile([P, 2, FEAT], BF16)
+        nc.vector.memset(vectors[:], 0.0)
         nc.scalar.dma_start(out=vectors[0:1, GAMMA, :], in_=gamma_e.rearrange("(o n) -> o n", o=1))
         nc.scalar.dma_start(out=vectors[0:1, BETA, :], in_=beta_e.rearrange("(o n) -> o n", o=1))
         ones = const.tile([P, P], BF16)
@@ -99,6 +103,11 @@ def tile_densegatlayer_pb_kernel(
         nc.vector.memset(eps[:], LN_EPS)
         identity = const.tile([P, P], F32)
         make_identity(nc, identity[:])
+
+        table_warmer = const.tile([P, 1], F32)
+        nc.scalar.activation(
+            out=table_warmer[:], in_=eps[:], func=ACT.Abs_reciprocal_sqrt, bias=eps[:, 0:1], scale=1.0
+        )
 
         node_psum = psum_xt.tile([P, 2, 2, P], F32, tag="xt")
         for u in range(2):
@@ -109,25 +118,6 @@ def tile_densegatlayer_pb_kernel(
             )
         node_words = const.tile([P, 2, P], F32)
         nc.scalar.copy(out=node_words[:], in_=node_psum[:, 0, :, :])
-
-        def spread(which):
-            psum_tile = psum_rows.tile([P, FEAT], F32, tag="by_rows")
-            nc.tensor.matmul(
-                out=psum_tile[:], lhsT=ones[:], rhs=vectors[:, which, :], start=True, stop=True
-            )
-            return psum_tile
-
-        mask_all = spread(MASK)
-        bias_all = spread(BIAS)
-        gain_shift = psum_const.tile([P, 2, FEAT], BF16)
-        for slot, which in enumerate((GAMMA, BETA)):
-            nc.tensor.matmul(
-                out=gain_shift[:, slot, :], lhsT=ones[:], rhs=vectors[:, which, :], start=True, stop=True
-            )
-        gamma_all = gain_shift[:, 0, :]
-        beta_all = gain_shift[:, 1, :]
-        gain_shift_sbuf = const.tile([P, 2, FEAT], F32)
-        nc.vector.tensor_copy(out=gain_shift_sbuf[:], in_=gain_shift[:])
 
         is_i = const.tile([P, I_PER_CHUNK], F32)
         nc.vector.tensor_reduce(
@@ -143,23 +133,24 @@ def tile_densegatlayer_pb_kernel(
             axis=AXIS_X,
             op=ALU.add,
         )
-        mask_values = mask_all[:, 0 : GRAPHS * NODES]
+        first_columns = const.tile([P, FEATURE_BLOCKS], BF16)
+        nc.vector.tensor_copy(out=first_columns[:], in_=identity[:, 0:FEATURE_BLOCKS])
         picked_i = const.tile([P, CHUNKS, I_PER_CHUNK], F32)
         nc.vector.tensor_tensor(
             out=picked_i[:],
-            in0=mask_values.rearrange("p (c a) -> p c a", a=I_PER_CHUNK),
+            in0=mask_all[:].rearrange("p (c a) -> p c a", a=I_PER_CHUNK),
             in1=is_i[:].unsqueeze(1).to_broadcast([P, CHUNKS, I_PER_CHUNK]),
+            op=ALU.mult,
+        )
+        picked_j = const.tile([P, GRAPHS * TILES, J_GROUPS], F32)
+        nc.vector.tensor_tensor(
+            out=picked_j[:].rearrange("p (b t) g -> p b t g", t=TILES),
+            in0=mask_all[:].rearrange("p (b g t) -> p b t g", b=GRAPHS, t=TILES),
+            in1=is_j[:].unsqueeze(1).unsqueeze(1).to_broadcast([P, GRAPHS, TILES, J_GROUPS]),
             op=ALU.mult,
         )
         mask_i = const.tile([P, CHUNKS], F32)
         nc.vector.tensor_reduce(out=mask_i[:], in_=picked_i[:], axis=AXIS_X, op=ALU.add)
-        picked_j = const.tile([P, GRAPHS * TILES, J_GROUPS], F32)
-        nc.vector.tensor_tensor(
-            out=picked_j[:].rearrange("p (b t) g -> p b t g", t=TILES),
-            in0=mask_values.rearrange("p (b g t) -> p b t g", b=GRAPHS, t=TILES),
-            in1=is_j[:].unsqueeze(1).unsqueeze(1).to_broadcast([P, GRAPHS, TILES, J_GROUPS]),
-            op=ALU.mult,
-        )
         mask_j = const.tile([P, GRAPHS * TILES], F32)
         nc.vector.tensor_reduce(out=mask_j[:], in_=picked_j[:], axis=AXIS_X, op=ALU.add)
         e_mask = const.tile([P, CHUNKS, TILES], F32)
@@ -176,15 +167,35 @@ def tile_densegatlayer_pb_kernel(
             op=ALU.mult,
         )
 
-        picked_bias = const.tile([P, FEATURE_BLOCKS, P], F32)
-        nc.vector.tensor_tensor(
-            out=picked_bias[:],
-            in0=bias_all[:].rearrange("p (f q) -> p f q", q=P),
-            in1=identity[:].unsqueeze(1).to_broadcast([P, FEATURE_BLOCKS, P]),
-            op=ALU.mult,
-        )
         bias_column = const.tile([P, FEATURE_BLOCKS], F32)
-        nc.vector.tensor_reduce(out=bias_column[:], in_=picked_bias[:], axis=AXIS_X, op=ALU.add)
+        gain_shift = psum_const.tile([P, 2, FEAT], BF16)
+        gamma_all = gain_shift[:, GAMMA, :]
+        beta_all = gain_shift[:, BETA, :]
+        gain_shift_sbuf = const.tile([P, 2, FEAT], F32)
+
+        def spread_bias():
+            bias_psum = psum_rows.tile([P, FEAT], F32, tag="by_rows")
+            nc.tensor.matmul(
+                out=bias_psum[:, 0:FEATURE_BLOCKS],
+                lhsT=bias_rows[:],
+                rhs=first_columns[:],
+                start=True,
+                stop=True,
+            )
+            nc.scalar.copy(out=bias_column[:], in_=bias_psum[:, 0:FEATURE_BLOCKS])
+
+        def spread_gain_shift():
+            for which in (GAMMA, BETA):
+                nc.tensor.matmul(
+                    out=gain_shift[:, which, :],
+                    lhsT=ones[:],
+                    rhs=vectors[:, which, :],
+                    start=True,
+                    stop=True,
+                )
+
+        def copy_gain_shift():
+            nc.vector.tensor_copy(out=gain_shift_sbuf[:], in_=gain_shift[:])
 
         row_codes = const.tile([P, GRAPHS, CHUNKS_PER_GRAPH * P], U32, align_bytes=64)
         row_planes = const.tile([P, GRAPHS, CHUNKS_PER_GRAPH * P], U8, align_bytes=64)
@@ -384,9 +395,12 @@ def tile_densegatlayer_pb_kernel(
             square_tiles[j] = squares
 
         def on_gpsimd(j, a):
-            if j // 2 == CHUNKS - 1:
-                return j % 2 == 0 and a == 1
-            return PAIR * (j % 2) + a in GPSIMD_TILES
+            c, t = j // 2, PAIR * (j % 2) + a
+            if c == CHUNKS - 1:
+                return t == 1
+            if c % 4 == 3 and t == 1:
+                return True
+            return t in GPSIMD_TILES
 
         def centre_and_gain(j):
             scaled = row_pool.tile([P, PAIR, FEAT], F32)
@@ -463,11 +477,14 @@ def tile_densegatlayer_pb_kernel(
         def pair(j):
             return 0 <= j < PAIRS
 
-        VECTOR_MASKS = 4
+        VECTOR_MASKS = 12
 
-        for h in range(-9, PAIRS + 6):
-            if h % 2 != 0 and 1 <= (h + 9) // 2 < CHUNKS:
-                load((h + 9) // 2)
+        MASK_LEAD = 13
+        LOAD_LEAD = MASK_LEAD + 4
+
+        for h in range(-LOAD_LEAD, PAIRS + 6):
+            if h % 2 != 0 and 1 <= (h + LOAD_LEAD) // 2 < CHUNKS:
+                load((h + LOAD_LEAD) // 2)
             if -5 <= h <= -3:
                 mask(h + 5, True)
             if h == -4:
@@ -477,6 +494,9 @@ def tile_densegatlayer_pb_kernel(
             if h == -2:
                 quantise_row_nodes(0, 0, 1)
                 quantise_col_nodes(0)
+                spread_bias()
+            if h == -1:
+                spread_gain_shift()
             if pair(h - 3):
                 add_residual(h - 3)
             if pair(h + 2):
@@ -509,14 +529,18 @@ def tile_densegatlayer_pb_kernel(
                 quantise_row_nodes(1, 0, TILES)
             if h % 2 != 0 and pair(h + 1):
                 quantise((h + 1) // 2)
-            if h == -1:
-                mask(VECTOR_MASKS - 1, True)
             if -1 <= h <= 1:
                 copy_row_nodes(0, h + 2, nc.scalar.copy)
             if h == 0:
                 quantise_row_nodes(0, 1, 1)
+                copy_gain_shift()
             if h == 2:
                 quantise_row_nodes(0, 2, 2)
+            if h == -1:
+                mask(3, True)
+            if -1 <= h <= 2:
+                mask(2 * h + 6, True)
+                mask(2 * h + 7, True)
             if pair(h - 4):
                 centre_and_gain(h - 4)
             if pair(h - 5):
@@ -525,8 +549,8 @@ def tile_densegatlayer_pb_kernel(
                 to_rows(h - 2)
             if pair(h + 3):
                 transpose(h + 3)
-            if pair(h + 5) and h + 5 >= VECTOR_MASKS:
-                mask(h + 5, False)
+            if pair(h + MASK_LEAD) and h + MASK_LEAD >= VECTOR_MASKS:
+                mask(h + MASK_LEAD, False)
             if pair(h - 5):
                 normalise_on_gpsimd(h - 5)
                 store(h - 5)

@@ -48,7 +48,7 @@ def tile_densegatlayer_pb_kernel(
         tc.manual_schedule(),
         tc.tile_pool(name="const", bufs=1) as const,
         tc.tile_pool(name="emb", bufs=11) as emb_pool,
-        tc.tile_pool(name="xe", bufs=12) as xe_pool,
+        tc.tile_pool(name="xe", bufs=20) as xe_pool,
         tc.tile_pool(name="stage", bufs=2) as stage,
         tc.tile_pool(name="features", bufs=3) as feature_pool,
         tc.tile_pool(name="rows", bufs=4) as row_pool,
@@ -251,16 +251,20 @@ def tile_densegatlayer_pb_kernel(
         y_tiles, minus_mean_tiles, square_tiles, rstd_tiles, scaled_tiles = {}, {}, {}, {}, {}
         squares_unread = const.tile([P, FEAT], BF16)
 
-        def mask(j, on_vector):
+        def mask(j, engine):
             c, half = divmod(j, 2)
             xe = xe_pool.tile([P, PAIR, FEAT], BF16)
             for a in range(PAIR):
                 t = PAIR * half + a
                 xe_words = xe[:, a, :].rearrange("p (u w e) -> p u w e", u=2, e=2)
                 emb_words = emb_tiles[c][:, t, :].rearrange("p (w u e) -> p u w e", u=2, e=2)
-                if on_vector:
+                if engine == "vector":
                     nc.vector.tensor_scalar_mul(
                         out=xe_words, in0=emb_words, scalar1=e_mask[:, c, t : t + 1]
+                    )
+                elif engine == "scalar":
+                    nc.scalar.activation(
+                        out=xe_words, in_=emb_words, func=ACT.Copy, scale=e_mask[:, c, t : t + 1]
                     )
                 else:
                     nc.gpsimd.tensor_scalar(
@@ -478,6 +482,7 @@ def tile_densegatlayer_pb_kernel(
             return 0 <= j < PAIRS
 
         VECTOR_MASKS = 12
+        SCALAR_MASKS = 4
 
         MASK_LEAD = 13
         LOAD_LEAD = MASK_LEAD + 4
@@ -486,7 +491,7 @@ def tile_densegatlayer_pb_kernel(
             if h % 2 != 0 and 1 <= (h + LOAD_LEAD) // 2 < CHUNKS:
                 load((h + LOAD_LEAD) // 2)
             if -5 <= h <= -3:
-                mask(h + 5, True)
+                mask(h + 5, "vector")
             if h == -4:
                 copy_row_nodes(0, 0, nc.scalar.copy)
                 for t in range(TILES):
@@ -537,10 +542,12 @@ def tile_densegatlayer_pb_kernel(
             if h == 2:
                 quantise_row_nodes(0, 2, 2)
             if h == -1:
-                mask(3, True)
+                mask(3, "vector")
             if -1 <= h <= 2:
-                mask(2 * h + 6, True)
-                mask(2 * h + 7, True)
+                mask(2 * h + 6, "vector")
+                mask(2 * h + 7, "vector")
+            if 1 <= h < 2 * SCALAR_MASKS and h % 2 == 1:
+                mask(VECTOR_MASKS + h // 2, "scalar")
             if pair(h - 4):
                 centre_and_gain(h - 4)
             if pair(h - 5):
@@ -549,8 +556,8 @@ def tile_densegatlayer_pb_kernel(
                 to_rows(h - 2)
             if pair(h + 3):
                 transpose(h + 3)
-            if pair(h + MASK_LEAD) and h + MASK_LEAD >= VECTOR_MASKS:
-                mask(h + MASK_LEAD, False)
+            if pair(h + MASK_LEAD) and h + MASK_LEAD >= VECTOR_MASKS + SCALAR_MASKS:
+                mask(h + MASK_LEAD, "gpsimd")
             if pair(h - 5):
                 normalise_on_gpsimd(h - 5)
                 store(h - 5)

@@ -484,11 +484,23 @@ def tile_densegatlayer_pb_kernel(
         VECTOR_MASKS = 12
         SCALAR_MASKS = 4
 
-        MASK_LEAD = 13
-        LOAD_LEAD = MASK_LEAD + 4
+        GPSIMD_FIRST = VECTOR_MASKS + SCALAR_MASKS
+        EARLY_MASKS = 6
+
+        def gpsimd_masks(h):
+            if -1 <= h < EARLY_MASKS - 1:
+                return [GPSIMD_FIRST + h + 1]
+            if h >= 8 and h % 2 == 0 and pair(GPSIMD_FIRST + EARLY_MASKS + (h - 8) // 2):
+                return [GPSIMD_FIRST + EARLY_MASKS + (h - 8) // 2]
+            return []
+
+        LOAD_LEAD = 17
+        EMB_BUFFERS = 11
+        for c in range(1, EMB_BUFFERS):
+            load(c)
 
         for h in range(-LOAD_LEAD, PAIRS + 6):
-            if h % 2 != 0 and 1 <= (h + LOAD_LEAD) // 2 < CHUNKS:
+            if h % 2 != 0 and EMB_BUFFERS <= (h + LOAD_LEAD) // 2 < CHUNKS:
                 load((h + LOAD_LEAD) // 2)
             if -5 <= h <= -3:
                 mask(h + 5, "vector")
@@ -556,8 +568,8 @@ def tile_densegatlayer_pb_kernel(
                 to_rows(h - 2)
             if pair(h + 3):
                 transpose(h + 3)
-            if pair(h + MASK_LEAD) and h + MASK_LEAD >= VECTOR_MASKS + SCALAR_MASKS:
-                mask(h + MASK_LEAD, "gpsimd")
             if pair(h - 5):
                 normalise_on_gpsimd(h - 5)
                 store(h - 5)
+            for j in gpsimd_masks(h):
+                mask(j, "gpsimd")

@@ -25,6 +25,7 @@ CHUNK_ROWS = P * TILES
 CHUNKS = GRAPHS * NODES * NODES // CHUNK_ROWS
 CHUNKS_PER_GRAPH = CHUNKS // GRAPHS
 I_PER_CHUNK = CHUNK_ROWS // NODES
+REPEATS = 4
 J_GROUPS = NODES // TILES
 
 PAIR = 2
@@ -109,15 +110,14 @@ def tile_densegatlayer_pb_kernel(
             out=table_warmer[:], in_=eps[:], func=ACT.Abs_reciprocal_sqrt, bias=eps[:, 0:1], scale=1.0
         )
 
-        node_psum = psum_xt.tile([P, 2, 2, P], F32, tag="xt")
+        node_psum = psum_rows.tile([P, FEAT], F32, tag="by_rows")
         for u in range(2):
             nc.tensor.transpose(
-                out=node_psum[:, 0, u, :],
+                out=node_psum[:, u * P : (u + 1) * P],
                 in_=node_rows[:].bitcast(F32)[:, u:WORDS:2],
                 identity=identity[:],
             )
-        node_words = const.tile([P, 2, P], F32)
-        nc.scalar.copy(out=node_words[:], in_=node_psum[:, 0, :, :])
+        node_words = node_psum[:, 0 : 2 * P].rearrange("p (u n) -> p u n", u=2)
 
         is_i = const.tile([P, I_PER_CHUNK], F32)
         nc.vector.tensor_reduce(
@@ -202,49 +202,83 @@ def tile_densegatlayer_pb_kernel(
         col_codes = const.tile([P, GRAPHS, TILES * P], U32, align_bytes=64)
         col_planes = const.tile([P, GRAPHS, TILES * P], U8, align_bytes=64)
 
-        node_inputs = {}
-        NODES_PER_PIECE = NODES // TILES
+        node_col_in = const.tile([P, GRAPHS, NODES * PACK], BF16, align_bytes=64)
+        node_row_in = const.tile([P, GRAPHS, NODES * REPEATS * PACK], BF16, align_bytes=64)
+        node_col_codes = const.tile([P, GRAPHS, NODES], U32, align_bytes=64)
+        node_row_codes = const.tile([P, GRAPHS, NODES * REPEATS], U32, align_bytes=64)
+        node_col_planes = const.tile([P, GRAPHS, NODES], U8, align_bytes=64)
+        nc.vector.memset(node_col_planes[:].bitcast(I32), 0)
+        node_row_planes = const.tile([P, GRAPHS, NODES * REPEATS], U8, align_bytes=64)
+        nc.vector.memset(node_row_planes[:].bitcast(I32), 0)
 
-        def copy_row_nodes(b, piece, copy):
-            if piece == 0:
-                row_in = stage.tile([P, NODES * J_GROUPS * PACK], BF16, align_bytes=64)
-                col_in = stage.tile([P, TILES * P * PACK], BF16, align_bytes=64)
-                node_inputs[b] = (row_in, col_in)
-            first = piece * NODES_PER_PIECE
-            copy(
-                out=node_inputs[b][0][:]
-                .bitcast(F32)
-                .rearrange("p (n g u) -> p n g u", g=J_GROUPS, u=2)[:, first : first + NODES_PER_PIECE],
-                in_=node_words[:, :, b * NODES + first : b * NODES + first + NODES_PER_PIECE]
+        def copy_nodes(b):
+            nc.scalar.copy(
+                out=node_col_in[:, b, :].bitcast(F32).rearrange("p (t g u) -> p t g u", t=TILES, u=2),
+                in_=node_words[:, :, b * NODES : (b + 1) * NODES].rearrange(
+                    "p u (g t) -> p t g u", t=TILES
+                ),
+            )
+            nc.scalar.copy(
+                out=node_row_in[:, b, :].bitcast(F32).rearrange("p (n r u) -> p n r u", r=REPEATS, u=2),
+                in_=node_words[:, :, b * NODES : (b + 1) * NODES]
                 .rearrange("p u n -> p n u")
                 .unsqueeze(2)
-                .to_broadcast([P, NODES_PER_PIECE, J_GROUPS, 2]),
+                .to_broadcast([P, NODES, REPEATS, 2]),
             )
 
-        def copy_col_nodes(b, t, copy):
-            copy(
-                out=node_inputs[b][1][:]
-                .bitcast(F32)
-                .rearrange("p (t a g u) -> p t a g u", t=TILES, a=I_PER_CHUNK, u=2)[:, t],
-                in_=node_words[:, :, b * NODES + t : (b + 1) * NODES : TILES]
-                .rearrange("p u g -> p g u")
-                .unsqueeze(1)
-                .to_broadcast([P, I_PER_CHUNK, J_GROUPS, 2]),
-            )
-
-        def quantise_col_nodes(b):
+        def quantise_nodes(b):
             nc.vector.quantize_mx(
-                out=col_codes[:, b, :].bitcast(FP8X4),
-                scales=col_planes[:, b, :],
-                in_=node_inputs[b][1][:],
+                out=node_col_codes[:, b, :].bitcast(FP8X4),
+                scales=node_col_planes[:, b, :],
+                in_=node_col_in[:, b, :],
+            )
+            nc.vector.quantize_mx(
+                out=node_row_codes[:, b, :].bitcast(FP8X4),
+                scales=node_row_planes[:, b, :],
+                in_=node_row_in[:, b, :],
             )
 
-        def quantise_row_nodes(b, first, pieces):
-            cols = slice(first * NODES_PER_PIECE * J_GROUPS, (first + pieces) * NODES_PER_PIECE * J_GROUPS)
-            nc.vector.quantize_mx(
-                out=row_codes[:, b, cols].bitcast(FP8X4),
-                scales=row_planes[:, b, cols],
-                in_=node_inputs[b][0][:, PACK * cols.start : PACK * cols.stop],
+        def spread_col_nodes(b):
+            nc.vector.tensor_copy(
+                out=col_codes[:, b, :]
+                .bitcast(I32)
+                .rearrange("p (t a g) -> p t a g", t=TILES, a=I_PER_CHUNK),
+                in_=node_col_codes[:, b, :]
+                .bitcast(I32)
+                .rearrange("p (t g) -> p t g", t=TILES)
+                .unsqueeze(2)
+                .to_broadcast([P, TILES, I_PER_CHUNK, J_GROUPS]),
+            )
+            nc.vector.tensor_copy(
+                out=col_planes[:, b, :]
+                .bitcast(I32)
+                .rearrange("p (t a w) -> p t a w", t=TILES, a=I_PER_CHUNK),
+                in_=node_col_planes[:, b, :]
+                .bitcast(I32)
+                .rearrange("p (t w) -> p t w", t=TILES)
+                .unsqueeze(2)
+                .to_broadcast([P, TILES, I_PER_CHUNK, J_GROUPS // 4]),
+            )
+
+        def spread_row_nodes(b, first, chunks):
+            nodes = slice(first * I_PER_CHUNK, (first + chunks) * I_PER_CHUNK)
+            cols = slice(first * P, (first + chunks) * P)
+            small = slice(nodes.start * REPEATS, nodes.stop * REPEATS)
+            copies = J_GROUPS // REPEATS
+            nc.vector.tensor_copy(
+                out=row_codes[:, b, cols].bitcast(I32).rearrange("p (n q r) -> p n q r", q=copies, r=REPEATS),
+                in_=node_row_codes[:, b, small]
+                .bitcast(I32)
+                .rearrange("p (n r) -> p n r", r=REPEATS)
+                .unsqueeze(2)
+                .to_broadcast([P, chunks * I_PER_CHUNK, copies, REPEATS]),
+            )
+            nc.vector.tensor_copy(
+                out=row_planes[:, b, cols].bitcast(I32).rearrange("p (n q) -> p n q", q=copies),
+                in_=node_row_planes[:, b, small]
+                .bitcast(I32)
+                .unsqueeze(2)
+                .to_broadcast([P, chunks * I_PER_CHUNK, copies]),
             )
 
         xe_tiles, xt_tiles, grouped_tiles, code_tiles, feature_tiles, edge_tiles = {}, {}, {}, {}, {}, {}
@@ -505,12 +539,11 @@ def tile_densegatlayer_pb_kernel(
             if -5 <= h <= -3:
                 mask(h + 5, "vector")
             if h == -4:
-                copy_row_nodes(0, 0, nc.scalar.copy)
-                for t in range(TILES):
-                    copy_col_nodes(0, t, nc.vector.tensor_copy if t < PAIR else nc.scalar.copy)
+                copy_nodes(0)
             if h == -2:
-                quantise_row_nodes(0, 0, 1)
-                quantise_col_nodes(0)
+                quantise_nodes(0)
+                spread_col_nodes(0)
+                spread_row_nodes(0, 0, 2)
                 spread_bias()
             if h == -1:
                 spread_gain_shift()
@@ -537,22 +570,20 @@ def tile_densegatlayer_pb_kernel(
                 copy_block(h // 2, first_block + 1)
             if pair(h - 4):
                 inverse_deviation(h - 4)
-            if 4 <= h < 4 + TILES:
-                copy_row_nodes(1, h - 4, nc.scalar.copy)
-            if 4 + TILES <= h < 4 + 2 * TILES:
-                copy_col_nodes(1, h - 4 - TILES, nc.scalar.copy)
-            if h == 4 + 2 * TILES:
-                quantise_col_nodes(1)
-                quantise_row_nodes(1, 0, TILES)
+            if h == 0:
+                copy_nodes(1)
+            if h == 9:
+                quantise_nodes(1)
+            if h == 10:
+                spread_col_nodes(1)
+            if 11 <= h < 15:
+                spread_row_nodes(1, 2 * (h - 11), 2)
             if h % 2 != 0 and pair(h + 1):
                 quantise((h + 1) // 2)
-            if -1 <= h <= 1:
-                copy_row_nodes(0, h + 2, nc.scalar.copy)
             if h == 0:
-                quantise_row_nodes(0, 1, 1)
                 copy_gain_shift()
-            if h == 2:
-                quantise_row_nodes(0, 2, 2)
+            if h == 1:
+                spread_row_nodes(0, 2, 6)
             if h == -1:
                 mask(3, "vector")
             if -1 <= h <= 2:

@@ -515,17 +515,19 @@ def tile_densegatlayer_pb_kernel(
         def pair(j):
             return 0 <= j < PAIRS
 
-        VECTOR_MASKS = 12
-        SCALAR_MASKS = 4
+        VECTOR_MASKS = 16
 
-        GPSIMD_FIRST = VECTOR_MASKS + SCALAR_MASKS
         EARLY_MASKS = 6
+        LATE_FIRST = VECTOR_MASKS + EARLY_MASKS
+        SCALAR_MASKS = [j for j in range(LATE_FIRST, PAIRS - 2) if j % 2 == 1]
+        LATE_GPSIMD = [j for j in range(LATE_FIRST, PAIRS) if j not in SCALAR_MASKS]
+        SCALAR_LEAD = 6
 
         def gpsimd_masks(h):
             if -1 <= h < EARLY_MASKS - 1:
-                return [GPSIMD_FIRST + h + 1]
-            if h >= 8 and h % 2 == 0 and pair(GPSIMD_FIRST + EARLY_MASKS + (h - 8) // 2):
-                return [GPSIMD_FIRST + EARLY_MASKS + (h - 8) // 2]
+                return [VECTOR_MASKS + h + 1]
+            if h >= 8 and h % 3 == 2:
+                return LATE_GPSIMD[(h - 8) // 3 : (h - 8) // 3 + 1]
             return []
 
         LOAD_LEAD = 17
@@ -586,11 +588,11 @@ def tile_densegatlayer_pb_kernel(
                 spread_row_nodes(0, 2, 6)
             if h == -1:
                 mask(3, "vector")
-            if -1 <= h <= 2:
+            if -1 <= h <= 4:
                 mask(2 * h + 6, "vector")
                 mask(2 * h + 7, "vector")
-            if 1 <= h < 2 * SCALAR_MASKS and h % 2 == 1:
-                mask(VECTOR_MASKS + h // 2, "scalar")
+            if h + SCALAR_LEAD in SCALAR_MASKS:
+                mask(h + SCALAR_LEAD, "scalar")
             if pair(h - 4):
                 centre_and_gain(h - 4)
             if pair(h - 5):

@@ -515,17 +515,13 @@ def tile_densegatlayer_pb_kernel(
         def pair(j):
             return 0 <= j < PAIRS
 
-        VECTOR_MASKS = 16
+        VECTOR_MASKS = 22
 
-        EARLY_MASKS = 6
-        LATE_FIRST = VECTOR_MASKS + EARLY_MASKS
-        SCALAR_MASKS = [j for j in range(LATE_FIRST, PAIRS - 2) if j % 2 == 1]
-        LATE_GPSIMD = [j for j in range(LATE_FIRST, PAIRS) if j not in SCALAR_MASKS]
+        SCALAR_MASKS = [j for j in range(VECTOR_MASKS, PAIRS - 2) if j % 2 == 1]
+        LATE_GPSIMD = [j for j in range(VECTOR_MASKS, PAIRS) if j not in SCALAR_MASKS]
         SCALAR_LEAD = 6
 
         def gpsimd_masks(h):
-            if -1 <= h < EARLY_MASKS - 1:
-                return [VECTOR_MASKS + h + 1]
             if h >= 8 and h % 3 == 2:
                 return LATE_GPSIMD[(h - 8) // 3 : (h - 8) // 3 + 1]
             return []
@@ -586,11 +582,9 @@ def tile_densegatlayer_pb_kernel(
                 copy_gain_shift()
             if h == 1:
                 spread_row_nodes(0, 2, 6)
-            if h == -1:
-                mask(3, "vector")
-            if -1 <= h <= 4:
-                mask(2 * h + 6, "vector")
-                mask(2 * h + 7, "vector")
+            if -1 <= h <= 2:
+                for j in range(3 + 5 * (h + 1), min(3 + 5 * (h + 2), VECTOR_MASKS)):
+                    mask(j, "vector")
             if h + SCALAR_LEAD in SCALAR_MASKS:
                 mask(h + SCALAR_LEAD, "scalar")
             if pair(h - 4):

@@ -59,21 +59,33 @@ def tile_densegatlayer_pb_kernel(
         tc.psum_pool(name="psum_features", bufs=2) as psum_features,
         tc.psum_pool(name="psum_rows", bufs=4) as psum_rows,
     ):
-        mask_all = const.tile([P, GRAPHS * NODES], BF16)
-        nc.scalar.dma_start(
-            out=mask_all[:], in_=node_mask.rearrange("b n -> (b n)").partition_broadcast(P)
+        eps = const.tile([P, 1], F32)
+        nc.vector.memset(eps[:], LN_EPS)
+        mask_rows = const.tile([P, I_PER_CHUNK], BF16)
+        nc.vector.memset(mask_rows[:], 0.0)
+        mask_cols = const.tile([P, GRAPHS * TILES], BF16)
+        nc.vector.memset(mask_cols[:], 0.0)
+        nc.sync.dma_start(
+            out=mask_rows[0:CHUNKS, :], in_=node_mask.rearrange("b (c a) -> (b c) a", a=I_PER_CHUNK)
+        )
+        nc.sync.dma_start(
+            out=mask_cols[0:J_GROUPS, :].rearrange("g (b t) -> g b t", b=GRAPHS),
+            in_=node_mask.rearrange("b (g t) -> g b t", t=TILES),
         )
         node_rows = const.tile([P, FEAT], BF16)
         nc.sync.dma_start(out=node_rows[:], in_=new_node.flatten_outer_dims())
 
         emb_tiles = {}
 
-        def load(c):
+        def load(c, parts=1):
             emb = emb_pool.tile([P, TILES, FEAT], BF16)
-            nc.sync.dma_start(out=emb[:], in_=emb_chunks[c])
+            step = TILES // parts
+            for part in range(parts):
+                rows = slice(part * step, (part + 1) * step)
+                nc.sync.dma_start(out=emb[:, rows, :], in_=emb_chunks[c][:, rows, :])
             emb_tiles[c] = emb
 
-        load(0)
+        load(0, parts=2)
 
         w_planes = const.tile([P, 3, FEAT], U8, align_bytes=64)
         nc.vector.memset(w_planes[:].bitcast(I32), 0)
@@ -90,24 +102,65 @@ def tile_densegatlayer_pb_kernel(
 
         bias_rows = const.tile([P, P], BF16)
         nc.vector.memset(bias_rows[:], 0.0)
-        nc.scalar.dma_start(
+        nc.sync.dma_start(
             out=bias_rows[0:FEATURE_BLOCKS, :], in_=bedge.rearrange("(f q) -> f q", q=P)
         )
         GAMMA, BETA = 0, 1
         vectors = const.tile([P, 2, FEAT], BF16)
         nc.vector.memset(vectors[:], 0.0)
-        nc.scalar.dma_start(out=vectors[0:1, GAMMA, :], in_=gamma_e.rearrange("(o n) -> o n", o=1))
-        nc.scalar.dma_start(out=vectors[0:1, BETA, :], in_=beta_e.rearrange("(o n) -> o n", o=1))
+        nc.sync.dma_start(out=vectors[0:1, GAMMA, :], in_=gamma_e.rearrange("(o n) -> o n", o=1))
+        nc.sync.dma_start(out=vectors[0:1, BETA, :], in_=beta_e.rearrange("(o n) -> o n", o=1))
         ones = const.tile([P, P], BF16)
         nc.vector.memset(ones[:], 1.0)
-        eps = const.tile([P, 1], F32)
-        nc.vector.memset(eps[:], LN_EPS)
         identity = const.tile([P, P], F32)
         make_identity(nc, identity[:])
 
         table_warmer = const.tile([P, 1], F32)
         nc.scalar.activation(
             out=table_warmer[:], in_=eps[:], func=ACT.Abs_reciprocal_sqrt, bias=eps[:, 0:1], scale=1.0
+        )
+
+        first_columns = const.tile([P, J_GROUPS], BF16)
+        nc.vector.tensor_copy(out=first_columns[:], in_=identity[:, 0:J_GROUPS])
+        select_j = const.tile([P, I_PER_CHUNK, J_GROUPS], BF16)
+        nc.vector.tensor_copy(
+            out=select_j[:],
+            in_=first_columns[:].unsqueeze(1).to_broadcast([P, I_PER_CHUNK, J_GROUPS]),
+        )
+        spread_i = const.tile([P, I_PER_CHUNK, J_GROUPS], BF16)
+        nc.vector.tensor_copy(
+            out=spread_i[:],
+            in_=mask_rows[:].unsqueeze(2).to_broadcast([P, I_PER_CHUNK, J_GROUPS]),
+        )
+        mask_psum = psum_rows.tile([P, FEAT], F32, tag="by_rows")
+        nc.tensor.matmul(
+            out=mask_psum[:, CHUNKS : CHUNKS + GRAPHS * TILES],
+            lhsT=select_j[:].rearrange("p a g -> p (a g)"),
+            rhs=mask_cols[:],
+            start=True,
+            stop=True,
+        )
+        nc.tensor.matmul(
+            out=mask_psum[:, 0:CHUNKS],
+            lhsT=spread_i[:].rearrange("p a g -> p (a g)"),
+            rhs=first_columns[:],
+            start=True,
+            stop=True,
+        )
+        mask_j = const.tile([P, GRAPHS * TILES], F32)
+        nc.vector.tensor_copy(out=mask_j[:], in_=mask_psum[:, CHUNKS : CHUNKS + GRAPHS * TILES])
+        e_mask = const.tile([P, CHUNKS, TILES], F32)
+        nc.vector.tensor_tensor(
+            out=e_mask[:].rearrange("p (b c) t -> p b c t", b=GRAPHS),
+            in0=mask_psum[:, 0:CHUNKS]
+            .rearrange("p (b c) -> p b c", b=GRAPHS)
+            .unsqueeze(3)
+            .to_broadcast([P, GRAPHS, CHUNKS_PER_GRAPH, TILES]),
+            in1=mask_j[:]
+            .rearrange("p (b t) -> p b t", b=GRAPHS)
+            .unsqueeze(2)
+            .to_broadcast([P, GRAPHS, CHUNKS_PER_GRAPH, TILES]),
+            op=ALU.mult,
         )
 
         node_psum = psum_rows.tile([P, FEAT], F32, tag="by_rows")
@@ -118,54 +171,6 @@ def tile_densegatlayer_pb_kernel(
                 identity=identity[:],
             )
         node_words = node_psum[:, 0 : 2 * P].rearrange("p (u n) -> p u n", u=2)
-
-        is_i = const.tile([P, I_PER_CHUNK], F32)
-        nc.vector.tensor_reduce(
-            out=is_i[:],
-            in_=identity[:].rearrange("p (a g) -> p a g", g=J_GROUPS),
-            axis=AXIS_X,
-            op=ALU.add,
-        )
-        is_j = const.tile([P, J_GROUPS], F32)
-        nc.vector.tensor_reduce(
-            out=is_j[:],
-            in_=identity[:].rearrange("p (a g) -> p g a", g=J_GROUPS),
-            axis=AXIS_X,
-            op=ALU.add,
-        )
-        first_columns = const.tile([P, FEATURE_BLOCKS], BF16)
-        nc.vector.tensor_copy(out=first_columns[:], in_=identity[:, 0:FEATURE_BLOCKS])
-        picked_i = const.tile([P, CHUNKS, I_PER_CHUNK], F32)
-        nc.vector.tensor_tensor(
-            out=picked_i[:],
-            in0=mask_all[:].rearrange("p (c a) -> p c a", a=I_PER_CHUNK),
-            in1=is_i[:].unsqueeze(1).to_broadcast([P, CHUNKS, I_PER_CHUNK]),
-            op=ALU.mult,
-        )
-        picked_j = const.tile([P, GRAPHS * TILES, J_GROUPS], F32)
-        nc.vector.tensor_tensor(
-            out=picked_j[:].rearrange("p (b t) g -> p b t g", t=TILES),
-            in0=mask_all[:].rearrange("p (b g t) -> p b t g", b=GRAPHS, t=TILES),
-            in1=is_j[:].unsqueeze(1).unsqueeze(1).to_broadcast([P, GRAPHS, TILES, J_GROUPS]),
-            op=ALU.mult,
-        )
-        mask_i = const.tile([P, CHUNKS], F32)
-        nc.vector.tensor_reduce(out=mask_i[:], in_=picked_i[:], axis=AXIS_X, op=ALU.add)
-        mask_j = const.tile([P, GRAPHS * TILES], F32)
-        nc.vector.tensor_reduce(out=mask_j[:], in_=picked_j[:], axis=AXIS_X, op=ALU.add)
-        e_mask = const.tile([P, CHUNKS, TILES], F32)
-        nc.vector.tensor_tensor(
-            out=e_mask[:].rearrange("p (b c) t -> p b c t", b=GRAPHS),
-            in0=mask_i[:]
-            .rearrange("p (b c) -> p b c", b=GRAPHS)
-            .unsqueeze(3)
-            .to_broadcast([P, GRAPHS, CHUNKS_PER_GRAPH, TILES]),
-            in1=mask_j[:]
-            .rearrange("p (b t) -> p b t", b=GRAPHS)
-            .unsqueeze(2)
-            .to_broadcast([P, GRAPHS, CHUNKS_PER_GRAPH, TILES]),
-            op=ALU.mult,
-        )
 
         bias_column = const.tile([P, FEATURE_BLOCKS], F32)
         gain_shift = psum_const.tile([P, 2, FEAT], BF16)
@@ -178,7 +183,7 @@ def tile_densegatlayer_pb_kernel(
             nc.tensor.matmul(
                 out=bias_psum[:, 0:FEATURE_BLOCKS],
                 lhsT=bias_rows[:],
-                rhs=first_columns[:],
+                rhs=first_columns[:, 0:FEATURE_BLOCKS],
                 start=True,
                 stop=True,
             )
@@ -295,10 +300,6 @@ def tile_densegatlayer_pb_kernel(
                 if engine == "vector":
                     nc.vector.tensor_scalar_mul(
                         out=xe_words, in0=emb_words, scalar1=e_mask[:, c, t : t + 1]
-                    )
-                elif engine == "scalar":
-                    nc.scalar.activation(
-                        out=xe_words, in_=emb_words, func=ACT.Copy, scale=e_mask[:, c, t : t + 1]
                     )
                 else:
                     nc.gpsimd.tensor_scalar(
@@ -517,13 +518,9 @@ def tile_densegatlayer_pb_kernel(
 
         VECTOR_MASKS = 22
 
-        SCALAR_MASKS = [j for j in range(VECTOR_MASKS, PAIRS - 2) if j % 2 == 1]
-        LATE_GPSIMD = [j for j in range(VECTOR_MASKS, PAIRS) if j not in SCALAR_MASKS]
-        SCALAR_LEAD = 6
-
         def gpsimd_masks(h):
-            if h >= 8 and h % 3 == 2:
-                return LATE_GPSIMD[(h - 8) // 3 : (h - 8) // 3 + 1]
+            if h >= 8 and h % 2 == 0 and pair(VECTOR_MASKS + (h - 8) // 2):
+                return [VECTOR_MASKS + (h - 8) // 2]
             return []
 
         LOAD_LEAD = 17
@@ -585,8 +582,6 @@ def tile_densegatlayer_pb_kernel(
             if -1 <= h <= 2:
                 for j in range(3 + 5 * (h + 1), min(3 + 5 * (h + 2), VECTOR_MASKS)):
                     mask(j, "vector")
-            if h + SCALAR_LEAD in SCALAR_MASKS:
-                mask(h + SCALAR_LEAD, "scalar")
             if pair(h - 4):
                 centre_and_gain(h - 4)
             if pair(h - 5):

@@ -243,8 +243,8 @@ def tile_densegatlayer_pb_kernel(
                 in_=node_row_in[:, b, :],
             )
 
-        def spread_col_nodes(b):
-            nc.vector.tensor_copy(
+        def spread_col_nodes(b, copy):
+            copy(
                 out=col_codes[:, b, :]
                 .bitcast(I32)
                 .rearrange("p (t a g) -> p t a g", t=TILES, a=I_PER_CHUNK),
@@ -254,7 +254,7 @@ def tile_densegatlayer_pb_kernel(
                 .unsqueeze(2)
                 .to_broadcast([P, TILES, I_PER_CHUNK, J_GROUPS]),
             )
-            nc.vector.tensor_copy(
+            copy(
                 out=col_planes[:, b, :]
                 .bitcast(I32)
                 .rearrange("p (t a w) -> p t a w", t=TILES, a=I_PER_CHUNK),
@@ -265,12 +265,12 @@ def tile_densegatlayer_pb_kernel(
                 .to_broadcast([P, TILES, I_PER_CHUNK, J_GROUPS // 4]),
             )
 
-        def spread_row_nodes(b, first, chunks):
+        def spread_row_nodes(b, first, chunks, copy):
             nodes = slice(first * I_PER_CHUNK, (first + chunks) * I_PER_CHUNK)
             cols = slice(first * P, (first + chunks) * P)
             small = slice(nodes.start * REPEATS, nodes.stop * REPEATS)
             copies = J_GROUPS // REPEATS
-            nc.vector.tensor_copy(
+            copy(
                 out=row_codes[:, b, cols].bitcast(I32).rearrange("p (n q r) -> p n q r", q=copies, r=REPEATS),
                 in_=node_row_codes[:, b, small]
                 .bitcast(I32)
@@ -278,7 +278,7 @@ def tile_densegatlayer_pb_kernel(
                 .unsqueeze(2)
                 .to_broadcast([P, chunks * I_PER_CHUNK, copies, REPEATS]),
             )
-            nc.vector.tensor_copy(
+            copy(
                 out=row_planes[:, b, cols].bitcast(I32).rearrange("p (n q) -> p n q", q=copies),
                 in_=node_row_planes[:, b, small]
                 .bitcast(I32)
@@ -295,16 +295,14 @@ def tile_densegatlayer_pb_kernel(
             xe = xe_pool.tile([P, PAIR, FEAT], BF16)
             for a in range(PAIR):
                 t = PAIR * half + a
-                xe_words = xe[:, a, :].rearrange("p (u w e) -> p u w e", u=2, e=2)
-                emb_words = emb_tiles[c][:, t, :].rearrange("p (w u e) -> p u w e", u=2, e=2)
                 if engine == "vector":
                     nc.vector.tensor_scalar_mul(
-                        out=xe_words, in0=emb_words, scalar1=e_mask[:, c, t : t + 1]
+                        out=xe[:, a, :], in0=emb_tiles[c][:, t, :], scalar1=e_mask[:, c, t : t + 1]
                     )
                 else:
                     nc.gpsimd.tensor_scalar(
-                        out=xe_words,
-                        in0=emb_words,
+                        out=xe[:, a, :],
+                        in0=emb_tiles[c][:, t, :],
                         scalar1=e_mask[:, c, t : t + 1],
                         scalar2=1.0,
                         op0=ALU.mult,
@@ -318,7 +316,7 @@ def tile_densegatlayer_pb_kernel(
                 for u in range(2):
                     nc.tensor.transpose(
                         out=xt[:, a, u, :],
-                        in_=xe_tiles[j][:, a, :].bitcast(F32)[:, u * P : (u + 1) * P],
+                        in_=xe_tiles[j][:, a, :].bitcast(F32)[:, u:WORDS:2],
                         identity=identity[:],
                     )
             xt_tiles[j] = xt
@@ -519,8 +517,8 @@ def tile_densegatlayer_pb_kernel(
         VECTOR_MASKS = 22
 
         def gpsimd_masks(h):
-            if h >= 8 and h % 2 == 0 and pair(VECTOR_MASKS + (h - 8) // 2):
-                return [VECTOR_MASKS + (h - 8) // 2]
+            if h >= 7 and h % 2 != 0 and pair(VECTOR_MASKS + (h - 7) // 2):
+                return [VECTOR_MASKS + (h - 7) // 2]
             return []
 
         LOAD_LEAD = 17
@@ -537,8 +535,8 @@ def tile_densegatlayer_pb_kernel(
                 copy_nodes(0)
             if h == -2:
                 quantise_nodes(0)
-                spread_col_nodes(0)
-                spread_row_nodes(0, 0, 2)
+                spread_col_nodes(0, nc.vector.tensor_copy)
+                spread_row_nodes(0, 0, 2, nc.vector.tensor_copy)
                 spread_bias()
             if h == -1:
                 spread_gain_shift()
@@ -559,26 +557,22 @@ def tile_densegatlayer_pb_kernel(
                 multiply_block(h // 2, first_block + 1)
             if pair(h - 4):
                 sum_squares(h - 4, 1)
-            if pair(h - 3):
-                mean(h - 3)
+                inverse_deviation(h - 4)
             if pair(h):
                 copy_block(h // 2, first_block + 1)
-            if pair(h - 4):
-                inverse_deviation(h - 4)
+            if pair(h - 3):
+                mean(h - 3)
             if h == 0:
                 copy_nodes(1)
-            if h == 9:
+                spread_row_nodes(0, 2, 6, nc.gpsimd.tensor_copy)
+            if h == 1:
                 quantise_nodes(1)
-            if h == 10:
-                spread_col_nodes(1)
-            if 11 <= h < 15:
-                spread_row_nodes(1, 2 * (h - 11), 2)
+                spread_col_nodes(1, nc.gpsimd.tensor_copy)
+                spread_row_nodes(1, 0, CHUNKS_PER_GRAPH, nc.gpsimd.tensor_copy)
             if h % 2 != 0 and pair(h + 1):
                 quantise((h + 1) // 2)
             if h == 0:
                 copy_gain_shift()
-            if h == 1:
-                spread_row_nodes(0, 2, 6)
             if -1 <= h <= 2:
                 for j in range(3 + 5 * (h + 1), min(3 + 5 * (h + 2), VECTOR_MASKS)):
                     mask(j, "vector")
@@ -590,8 +584,11 @@ def tile_densegatlayer_pb_kernel(
                 to_rows(h - 2)
             if pair(h + 3):
                 transpose(h + 3)
+            if h % 2 != 0:
+                for j in (h - 5, h - 4):
+                    if pair(j):
+                        normalise_on_gpsimd(j)
             if pair(h - 5):
-                normalise_on_gpsimd(h - 5)
                 store(h - 5)
             for j in gpsimd_masks(h):
                 mask(j, "gpsimd")

@@ -30,6 +30,19 @@ J_GROUPS = NODES // TILES
 
 PAIR = 2
 PAIRS = 2 * CHUNKS
+VREG = 0
+GMIN = 0
+GMAX = 10
+GL = 1
+LS = 0
+LR = 0
+SH = 0
+VR = 2
+RB = 6
+G2 = (1, 3)
+VHEAD = 14
+GEARLY = 6
+LATEV = 3
 GPSIMD_TILES = (3,)
 
 FEATURE_BLOCKS = FEAT // P
@@ -52,7 +65,7 @@ def tile_densegatlayer_pb_kernel(
         tc.tile_pool(name="xe", bufs=20) as xe_pool,
         tc.tile_pool(name="stage", bufs=2) as stage,
         tc.tile_pool(name="features", bufs=3) as feature_pool,
-        tc.tile_pool(name="rows", bufs=4) as row_pool,
+        tc.tile_pool(name="rows", bufs=RB) as row_pool,
         tc.tile_pool(name="stats", bufs=6) as stats,
         tc.psum_pool(name="psum_const", bufs=1) as psum_const,
         tc.psum_pool(name="psum_xt", bufs=1) as psum_xt,
@@ -108,6 +121,7 @@ def tile_densegatlayer_pb_kernel(
         GAMMA, BETA = 0, 1
         vectors = const.tile([P, 2, FEAT], BF16)
         nc.vector.memset(vectors[:], 0.0)
+        load(1)
         nc.sync.dma_start(out=vectors[0:1, GAMMA, :], in_=gamma_e.rearrange("(o n) -> o n", o=1))
         nc.sync.dma_start(out=vectors[0:1, BETA, :], in_=beta_e.rearrange("(o n) -> o n", o=1))
         ones = const.tile([P, P], BF16)
@@ -200,7 +214,8 @@ def tile_densegatlayer_pb_kernel(
                 )
 
         def copy_gain_shift():
-            nc.vector.tensor_copy(out=gain_shift_sbuf[:], in_=gain_shift[:])
+            for which in (GAMMA, BETA):
+                nc.scalar.copy(out=gain_shift_sbuf[:, which, :], in_=gain_shift[:, which, :])
 
         row_codes = const.tile([P, GRAPHS, CHUNKS_PER_GRAPH * P], U32, align_bytes=64)
         row_planes = const.tile([P, GRAPHS, CHUNKS_PER_GRAPH * P], U8, align_bytes=64)
@@ -295,14 +310,20 @@ def tile_densegatlayer_pb_kernel(
             xe = xe_pool.tile([P, PAIR, FEAT], BF16)
             for a in range(PAIR):
                 t = PAIR * half + a
+                xe_words = xe[:, a, :].rearrange("p (u w e) -> p u w e", u=2, e=2)
+                emb_words = emb_tiles[c][:, t, :].rearrange("p (w u e) -> p u w e", u=2, e=2)
                 if engine == "vector":
                     nc.vector.tensor_scalar_mul(
-                        out=xe[:, a, :], in0=emb_tiles[c][:, t, :], scalar1=e_mask[:, c, t : t + 1]
+                        out=xe_words, in0=emb_words, scalar1=e_mask[:, c, t : t + 1]
+                    )
+                elif engine == "scalar":
+                    nc.scalar.activation(
+                        out=xe_words, in_=emb_words, func=ACT.Copy, scale=e_mask[:, c, t : t + 1]
                     )
                 else:
                     nc.gpsimd.tensor_scalar(
-                        out=xe[:, a, :],
-                        in0=emb_tiles[c][:, t, :],
+                        out=xe_words,
+                        in0=emb_words,
                         scalar1=e_mask[:, c, t : t + 1],
                         scalar2=1.0,
                         op0=ALU.mult,
@@ -311,15 +332,23 @@ def tile_densegatlayer_pb_kernel(
             xe_tiles[j] = xe
 
         def transpose(j):
-            xt = psum_xt.tile([P, PAIR, 2, P], F32, tag="xt")
+            if j in (1, 3):
+                free_bank = psum_rows.tile([P, FEAT], F32, tag="by_rows")
+                xt = free_bank[:].rearrange("p (a u r) -> p a u r", a=PAIR, u=2)
+            else:
+                xt_bank = psum_xt.tile([P, PAIR, 2, P], F32, tag="xt")
+                xt = xt_bank[:]
             for a in range(PAIR):
                 for u in range(2):
                     nc.tensor.transpose(
                         out=xt[:, a, u, :],
-                        in_=xe_tiles[j][:, a, :].bitcast(F32)[:, u:WORDS:2],
+                        in_=xe_tiles[j][:, a, :].bitcast(F32)[:, u * P : (u + 1) * P],
                         identity=identity[:],
                     )
             xt_tiles[j] = xt
+
+        def vector_regroups(j):
+            return VREG and j >= 6 and j % VREG == VR
 
         def regroup(j):
             c, half = divmod(j, 2)
@@ -329,9 +358,10 @@ def tile_densegatlayer_pb_kernel(
             grouped_words = (
                 grouped_tiles[c][:].bitcast(F32).rearrange("p (t r u) -> p t r u", t=TILES, u=2)
             )
-            nc.scalar.copy(
+            copy = nc.vector.tensor_copy if vector_regroups(j) else nc.scalar.copy
+            copy(
                 out=grouped_words[:, PAIR * half : PAIR * half + PAIR],
-                in_=xt_tiles[j][:].rearrange("p a u r -> p a r u"),
+                in_=xt_tiles[j].rearrange("p a u r -> p a r u"),
             )
 
         def quantise(c):
@@ -434,8 +464,8 @@ def tile_densegatlayer_pb_kernel(
         def on_gpsimd(j, a):
             c, t = j // 2, PAIR * (j % 2) + a
             if c == CHUNKS - 1:
-                return t == 1
-            if c % 4 == 3 and t == 1:
+                return t == GL
+            if c % 4 in G2 and t == 1 and GMIN <= c < GMAX:
                 return True
             return t in GPSIMD_TILES
 
@@ -507,49 +537,78 @@ def tile_densegatlayer_pb_kernel(
 
         def store(j):
             c, half = divmod(j, 2)
-            nc.sync.dma_start(
-                out=out_chunks[c][:, PAIR * half : PAIR * half + PAIR, :], in_=scaled_tiles[j][:]
-            )
+            pieces = PAIR if j == PAIRS - 1 else 1
+            width = PAIR // pieces
+            for a in range(0, PAIR, width):
+                nc.sync.dma_start(
+                    out=out_chunks[c][:, PAIR * half + a : PAIR * half + a + width, :],
+                    in_=scaled_tiles[j][:, a : a + width, :],
+                )
 
         def pair(j):
             return 0 <= j < PAIRS
 
-        VECTOR_MASKS = 22
+        LATE = list(range(VHEAD + GEARLY + SH, PAIRS))
+        LATE_V = [j for j in LATE if LATEV and j % LATEV == LATEV // 2]
+        LATE_S = [j for j in LATE if LS and j % LS == LR]
+        LATE_V = [j for j in LATE_V if j not in LATE_S]
+        LATE_G = [j for j in LATE if j not in LATE_V and j not in LATE_S]
+
+        def vector_masks(h):
+            if 0 <= h <= 1:
+                return [j for j in range(4 + 4 * h, 8 + 4 * h) if j < VHEAD]
+            if h == 2:
+                return list(range(12, VHEAD))
+            return [h + 9] if h + 9 in LATE_V else []
 
         def gpsimd_masks(h):
-            if h >= 7 and h % 2 != 0 and pair(VECTOR_MASKS + (h - 7) // 2):
-                return [VECTOR_MASKS + (h - 7) // 2]
+            if 0 <= h < GEARLY:
+                return [VHEAD + h]
+            if h >= 7 and h % 2 != 0:
+                return LATE_G[(h - 7) // 2 : (h - 7) // 2 + 1]
             return []
 
         LOAD_LEAD = 17
         EMB_BUFFERS = 11
-        for c in range(1, EMB_BUFFERS):
+        for c in range(2, EMB_BUFFERS):
             load(c)
+
+        mask(0, "vector")
+        copy_nodes(0)
+        transpose(0)
+        mask(1, "vector")
+        transpose(1)
+        regroup(0)
+        quantise_nodes(0)
+        spread_col_nodes(0, nc.vector.tensor_copy)
+        spread_row_nodes(0, 0, 2, nc.vector.tensor_copy)
+        regroup(1)
+        quantise(0)
+        copy_nodes(1)
+        spread_row_nodes(0, 2, 6, nc.vector.tensor_copy)
+        mask(2, "vector")
+        mask(3, "vector")
+        quantise_nodes(1)
+        spread_col_nodes(1, nc.vector.tensor_copy)
+        spread_row_nodes(1, 0, CHUNKS_PER_GRAPH, nc.vector.tensor_copy)
 
         for h in range(-LOAD_LEAD, PAIRS + 6):
             if h % 2 != 0 and EMB_BUFFERS <= (h + LOAD_LEAD) // 2 < CHUNKS:
                 load((h + LOAD_LEAD) // 2)
-            if -5 <= h <= -3:
-                mask(h + 5, "vector")
-            if h == -4:
-                copy_nodes(0)
-            if h == -2:
-                quantise_nodes(0)
-                spread_col_nodes(0, nc.vector.tensor_copy)
-                spread_row_nodes(0, 0, 2, nc.vector.tensor_copy)
-                spread_bias()
-            if h == -1:
-                spread_gain_shift()
+            if h >= 1 and pair(h + 2):
+                regroup(h + 2)
             if pair(h - 3):
                 add_residual(h - 3)
-            if pair(h + 2):
-                regroup(h + 2)
+            if h == 2:
+                copy_gain_shift()
             first_block = 2 * (h % 2)
             rows_first = h in (2, 3)
             if rows_first:
                 to_rows(h - 2)
             if pair(h):
                 multiply_block(h // 2, first_block)
+            if h == 0:
+                spread_bias()
             if pair(h - 4):
                 sum_squares(h - 4, 0)
             if pair(h):
@@ -562,28 +621,27 @@ def tile_densegatlayer_pb_kernel(
                 copy_block(h // 2, first_block + 1)
             if pair(h - 3):
                 mean(h - 3)
-            if h == 0:
-                copy_nodes(1)
-                spread_row_nodes(0, 2, 6, nc.gpsimd.tensor_copy)
-            if h == 1:
-                quantise_nodes(1)
-                spread_col_nodes(1, nc.gpsimd.tensor_copy)
-                spread_row_nodes(1, 0, CHUNKS_PER_GRAPH, nc.gpsimd.tensor_copy)
-            if h % 2 != 0 and pair(h + 1):
+            if h >= 0 and h % 2 != 0 and pair(h + 1):
                 quantise((h + 1) // 2)
-            if h == 0:
-                copy_gain_shift()
-            if -1 <= h <= 2:
-                for j in range(3 + 5 * (h + 1), min(3 + 5 * (h + 2), VECTOR_MASKS)):
-                    mask(j, "vector")
+            for j in vector_masks(h):
+                mask(j, "vector")
+            if h >= 0 and h + 9 in LATE_S:
+                mask(h + 9, "scalar")
+            if SH > 0 and 2 <= h < 2 + SH:
+                mask(VHEAD + GEARLY + h - 2, "scalar")
             if pair(h - 4):
                 centre_and_gain(h - 4)
             if pair(h - 5):
                 normalise(h - 5)
             if pair(h - 2) and not rows_first:
                 to_rows(h - 2)
-            if pair(h + 3):
+            if h == 0:
+                transpose(2)
+                regroup(2)
+            if h >= 0 and pair(h + 3):
                 transpose(h + 3)
+            if h == 1:
+                spread_gain_shift()
             if h % 2 != 0:
                 for j in (h - 5, h - 4):
                     if pair(j):

@@ -31,18 +31,29 @@ J_GROUPS = NODES // TILES
 PAIR = 2
 PAIRS = 2 * CHUNKS
 VREG = 0
-GMIN = 0
-GMAX = 10
+ST = 1
+GSKIP = 1
+UW = False
+GH = 3
+IL = True
+ML = 0
+QF = 99
+NG = 2
+GO = 1
+GT = 2
+V0 = 7
+GMIN = 2
+GMAX = 13
 GL = 1
 LS = 0
 LR = 0
 SH = 0
 VR = 2
 RB = 6
-G2 = (1, 3)
+G2 = (0, 2)
 VHEAD = 14
 GEARLY = 6
-LATEV = 3
+LATEV = 2
 GPSIMD_TILES = (3,)
 
 FEATURE_BLOCKS = FEAT // P
@@ -214,8 +225,7 @@ def tile_densegatlayer_pb_kernel(
                 )
 
         def copy_gain_shift():
-            for which in (GAMMA, BETA):
-                nc.scalar.copy(out=gain_shift_sbuf[:, which, :], in_=gain_shift[:, which, :])
+            nc.vector.tensor_copy(out=gain_shift_sbuf[:], in_=gain_shift[:])
 
         row_codes = const.tile([P, GRAPHS, CHUNKS_PER_GRAPH * P], U32, align_bytes=64)
         row_planes = const.tile([P, GRAPHS, CHUNKS_PER_GRAPH * P], U8, align_bytes=64)
@@ -305,13 +315,20 @@ def tile_densegatlayer_pb_kernel(
         y_tiles, minus_mean_tiles, square_tiles, rstd_tiles, scaled_tiles = {}, {}, {}, {}, {}
         squares_unread = const.tile([P, FEAT], BF16)
 
-        def mask(j, engine):
+        def mask(j, engine, tiles=(0, 1)):
             c, half = divmod(j, 2)
-            xe = xe_pool.tile([P, PAIR, FEAT], BF16)
-            for a in range(PAIR):
+            if j not in xe_tiles:
+                new_xe = xe_pool.tile([P, PAIR, FEAT], BF16)
+                xe_tiles[j] = new_xe
+            xe = xe_tiles[j]
+            for a in tiles:
                 t = PAIR * half + a
-                xe_words = xe[:, a, :].rearrange("p (u w e) -> p u w e", u=2, e=2)
-                emb_words = emb_tiles[c][:, t, :].rearrange("p (w u e) -> p u w e", u=2, e=2)
+                xe_words = xe[:, a, :].rearrange("p (u w e) -> p u w e", u=2, e=2) if UW else xe[:, a, :]
+                emb_words = (
+                    emb_tiles[c][:, t, :].rearrange("p (w u e) -> p u w e", u=2, e=2)
+                    if UW
+                    else emb_tiles[c][:, t, :]
+                )
                 if engine == "vector":
                     nc.vector.tensor_scalar_mul(
                         out=xe_words, in0=emb_words, scalar1=e_mask[:, c, t : t + 1]
@@ -329,7 +346,6 @@ def tile_densegatlayer_pb_kernel(
                         op0=ALU.mult,
                         op1=ALU.mult,
                     )
-            xe_tiles[j] = xe
 
         def transpose(j):
             if j in (1, 3):
@@ -342,7 +358,9 @@ def tile_densegatlayer_pb_kernel(
                 for u in range(2):
                     nc.tensor.transpose(
                         out=xt[:, a, u, :],
-                        in_=xe_tiles[j][:, a, :].bitcast(F32)[:, u * P : (u + 1) * P],
+                        in_=xe_tiles[j][:, a, :].bitcast(F32)[:, u * P : (u + 1) * P]
+                        if UW
+                        else xe_tiles[j][:, a, :].bitcast(F32)[:, u:WORDS:2],
                         identity=identity[:],
                     )
             xt_tiles[j] = xt
@@ -465,7 +483,7 @@ def tile_densegatlayer_pb_kernel(
             c, t = j // 2, PAIR * (j % 2) + a
             if c == CHUNKS - 1:
                 return t == GL
-            if c % 4 in G2 and t == 1 and GMIN <= c < GMAX:
+            if c % 4 in G2 and t == ST and GMIN <= c < GMAX:
                 return True
             return t in GPSIMD_TILES
 
@@ -505,22 +523,26 @@ def tile_densegatlayer_pb_kernel(
 
         def normalise_on_gpsimd(j):
             scaled = scaled_tiles[j]
-            for a in range(PAIR):
-                if on_gpsimd(j, a):
-                    nc.gpsimd.tensor_scalar(
-                        out=scaled[:, a, :],
-                        in0=y_tiles[j][0][:, a, :],
-                        scalar1=minus_mean_tiles[j][:, a : a + 1],
-                        scalar2=rstd_tiles[j][:, a : a + 1],
-                        op0=ALU.add,
-                        op1=ALU.mult,
-                    )
-                    nc.gpsimd.tensor_tensor(
-                        out=scaled[:, a, :], in0=scaled[:, a, :], in1=gain_shift_sbuf[:, 0, :], op=ALU.mult
-                    )
-                    nc.gpsimd.tensor_tensor(
-                        out=scaled[:, a, :], in0=scaled[:, a, :], in1=gain_shift_sbuf[:, 1, :], op=ALU.add
-                    )
+            tiles = [a for a in range(PAIR) if on_gpsimd(j, a)]
+            if not tiles:
+                return
+            for a in tiles:
+                nc.gpsimd.tensor_scalar(
+                    out=scaled[:, a, :],
+                    in0=y_tiles[j][0][:, a, :],
+                    scalar1=minus_mean_tiles[j][:, a : a + 1],
+                    scalar2=rstd_tiles[j][:, a : a + 1],
+                    op0=ALU.add,
+                    op1=ALU.mult,
+                )
+            both = scaled[:, tiles[0] : tiles[-1] + 1, :]
+            for which, op in ((0, ALU.mult), (1, ALU.add)):
+                nc.gpsimd.tensor_tensor(
+                    out=both,
+                    in0=both,
+                    in1=gain_shift_sbuf[:, which, :].unsqueeze(1).to_broadcast([P, len(tiles), FEAT]),
+                    op=op,
+                )
 
         def normalise(j):
             scaled = scaled_tiles[j]
@@ -535,37 +557,37 @@ def tile_densegatlayer_pb_kernel(
                         op1=ALU.add,
                     )
 
-        def store(j):
+        def store(j, tiles=(0, 1)):
             c, half = divmod(j, 2)
-            pieces = PAIR if j == PAIRS - 1 else 1
-            width = PAIR // pieces
-            for a in range(0, PAIR, width):
-                nc.sync.dma_start(
-                    out=out_chunks[c][:, PAIR * half + a : PAIR * half + a + width, :],
-                    in_=scaled_tiles[j][:, a : a + width, :],
-                )
+            first, last = tiles[0], tiles[-1]
+            nc.sync.dma_start(
+                out=out_chunks[c][:, PAIR * half + first : PAIR * half + last + 1, :],
+                in_=scaled_tiles[j][:, first : last + 1, :],
+            )
 
         def pair(j):
             return 0 <= j < PAIRS
 
-        LATE = list(range(VHEAD + GEARLY + SH, PAIRS))
-        LATE_V = [j for j in LATE if LATEV and j % LATEV == LATEV // 2]
-        LATE_S = [j for j in LATE if LS and j % LS == LR]
-        LATE_V = [j for j in LATE_V if j not in LATE_S]
-        LATE_G = [j for j in LATE if j not in LATE_V and j not in LATE_S]
+        LATE = list(range(VHEAD + GEARLY, PAIRS))
+        LATE_G = [LATE[0] + GO + 2 * i for i in range(NG)]
+        LATE_V = [j for j in LATE if j not in LATE_G]
+        G_SLOTS = [h for h in range(7, PAIRS) if h % 2 != 0 and not (GSKIP and ((h - 5) // 2) % 4 in G2)]
+        G_TILES = [(j, (a,)) for j in LATE_G for a in range(PAIR)] if GT == 1 else [(j, (0, 1)) for j in LATE_G]
 
         def vector_masks(h):
             if 0 <= h <= 1:
                 return [j for j in range(4 + 4 * h, 8 + 4 * h) if j < VHEAD]
             if h == 2:
                 return list(range(12, VHEAD))
-            return [h + 9] if h + 9 in LATE_V else []
+            if h >= V0 and h % 2 != 0:
+                return LATE_V[(h - V0) // 2 : (h - V0) // 2 + 1]
+            return []
 
         def gpsimd_masks(h):
             if 0 <= h < GEARLY:
-                return [VHEAD + h]
-            if h >= 7 and h % 2 != 0:
-                return LATE_G[(h - 7) // 2 : (h - 7) // 2 + 1]
+                return [(VHEAD + h, (0, 1))]
+            if h in G_SLOTS:
+                return G_TILES[G_SLOTS.index(h) : G_SLOTS.index(h) + 1]
             return []
 
         LOAD_LEAD = 17
@@ -595,11 +617,20 @@ def tile_densegatlayer_pb_kernel(
         for h in range(-LOAD_LEAD, PAIRS + 6):
             if h % 2 != 0 and EMB_BUFFERS <= (h + LOAD_LEAD) // 2 < CHUNKS:
                 load((h + LOAD_LEAD) // 2)
+            if ML == 1 and pair(h - 4):
+                mean(h - 4)
             if h >= 1 and pair(h + 2):
                 regroup(h + 2)
+            if ML == 2 and pair(h - 4):
+                mean(h - 4)
+            if h >= QF:
+                if h % 2 != 0 and pair(h + 1):
+                    quantise((h + 1) // 2)
+                for j in vector_masks(h):
+                    mask(j, "vector")
             if pair(h - 3):
                 add_residual(h - 3)
-            if h == 2:
+            if h == GH:
                 copy_gain_shift()
             first_block = 2 * (h % 2)
             rows_first = h in (2, 3)
@@ -609,26 +640,29 @@ def tile_densegatlayer_pb_kernel(
                 multiply_block(h // 2, first_block)
             if h == 0:
                 spread_bias()
-            if pair(h - 4):
+            if ML != 3 and pair(h - 4):
                 sum_squares(h - 4, 0)
             if pair(h):
                 copy_block(h // 2, first_block)
                 multiply_block(h // 2, first_block + 1)
+            if ML == 3 and pair(h - 4):
+                mean(h - 4)
+                sum_squares(h - 4, 0)
             if pair(h - 4):
                 sum_squares(h - 4, 1)
-                inverse_deviation(h - 4)
+                if not IL:
+                    inverse_deviation(h - 4)
             if pair(h):
                 copy_block(h // 2, first_block + 1)
-            if pair(h - 3):
+            if IL and pair(h - 4):
+                inverse_deviation(h - 4)
+            if ML == 0 and pair(h - 3):
                 mean(h - 3)
-            if h >= 0 and h % 2 != 0 and pair(h + 1):
-                quantise((h + 1) // 2)
-            for j in vector_masks(h):
-                mask(j, "vector")
-            if h >= 0 and h + 9 in LATE_S:
-                mask(h + 9, "scalar")
-            if SH > 0 and 2 <= h < 2 + SH:
-                mask(VHEAD + GEARLY + h - 2, "scalar")
+            if h < QF:
+                if h >= 0 and h % 2 != 0 and pair(h + 1):
+                    quantise((h + 1) // 2)
+                for j in vector_masks(h):
+                    mask(j, "vector")
             if pair(h - 4):
                 centre_and_gain(h - 4)
             if pair(h - 5):
@@ -646,7 +680,13 @@ def tile_densegatlayer_pb_kernel(
                 for j in (h - 5, h - 4):
                     if pair(j):
                         normalise_on_gpsimd(j)
-            if pair(h - 5):
+            if pair(h - 5) and h - 5 < PAIRS - 2:
                 store(h - 5)
-            for j in gpsimd_masks(h):
-                mask(j, "gpsimd")
+            if h - 5 == PAIRS - 2:
+                store(PAIRS - 2, (0,))
+            if h - 5 == PAIRS - 1:
+                store(PAIRS - 1, (0,))
+                store(PAIRS - 1, (1,))
+                store(PAIRS - 2, (1,))
+            for j, tiles in gpsimd_masks(h):
+                mask(j, "gpsimd", tiles)

import concourse.mybir as mybir
from concourse.masks import make_identity

F32 = mybir.dt.float32
BF16 = mybir.dt.bfloat16
I32 = mybir.dt.int32
U32 = mybir.dt.uint32
U8 = mybir.dt.uint8
FP8X4 = mybir.dt.float8_e4m3fn_x4
FP4X4 = mybir.dt.float4_e2m1fn_x4
ALU = mybir.AluOpType
ACT = mybir.ActivationFunctionType
AXIS_X = mybir.AxisListType.X

P = 128
GRAPHS = 2
NODES = 64
FEAT = 512
PACK = 4
WORDS = FEAT // 2
LN_EPS = 1e-5

TILES = 4
CHUNK_ROWS = P * TILES
CHUNKS = GRAPHS * NODES * NODES // CHUNK_ROWS
CHUNKS_PER_GRAPH = CHUNKS // GRAPHS
I_PER_CHUNK = CHUNK_ROWS // NODES
REPEATS = 4
J_GROUPS = NODES // TILES

PAIR = 2
PAIRS = 2 * CHUNKS
VREG = 0
ST = 1
GSKIP = 1
UW = False
GH = 3
IL = True
ML = 0
QF = 99
NG = 2
GO = 1
GT = 2
V0 = 7
GMIN = 2
GMAX = 13
GL = 1
LS = 0
LR = 0
SH = 0
VR = 2
RB = 6
G2 = (0, 2)
VHEAD = 14
GEARLY = 6
LATEV = 2
GPSIMD_TILES = (3,)

FEATURE_BLOCKS = FEAT // P
ROW_BLOCK, COL_BLOCK, EDGE_BLOCK = 0, 1, 2

FLOPS = 2 * FEAT * FEAT * (GRAPHS * NODES * NODES + 2 * GRAPHS * NODES)


def tile_densegatlayer_pb_kernel(
    tc, new_node, emb_edge, node_mask, Wedge_words, Wedge_scales, bedge, gamma_e, beta_e, out
):
    nc = tc.nc
    emb_chunks = emb_edge.flatten_outer_dims().rearrange("(c p t) k -> c p t k", p=P, t=TILES)
    out_chunks = out.flatten_outer_dims().rearrange("(c p t) k -> c p t k", p=P, t=TILES)

    with (
        tc.manual_schedule(),
        tc.tile_pool(name="const", bufs=1) as const,
        tc.tile_pool(name="emb", bufs=11) as emb_pool,
        tc.tile_pool(name="xe", bufs=20) as xe_pool,
        tc.tile_pool(name="stage", bufs=2) as stage,
        tc.tile_pool(name="features", bufs=3) as feature_pool,
        tc.tile_pool(name="rows", bufs=RB) as row_pool,
        tc.tile_pool(name="stats", bufs=6) as stats,
        tc.psum_pool(name="psum_const", bufs=1) as psum_const,
        tc.psum_pool(name="psum_xt", bufs=1) as psum_xt,
        tc.psum_pool(name="psum_features", bufs=2) as psum_features,
        tc.psum_pool(name="psum_rows", bufs=4) as psum_rows,
    ):
        eps = const.tile([P, 1], F32)
        nc.vector.memset(eps[:], LN_EPS)
        mask_rows = const.tile([P, I_PER_CHUNK], BF16)
        nc.vector.memset(mask_rows[:], 0.0)
        mask_cols = const.tile([P, GRAPHS * TILES], BF16)
        nc.vector.memset(mask_cols[:], 0.0)
        nc.sync.dma_start(
            out=mask_rows[0:CHUNKS, :], in_=node_mask.rearrange("b (c a) -> (b c) a", a=I_PER_CHUNK)
        )
        nc.sync.dma_start(
            out=mask_cols[0:J_GROUPS, :].rearrange("g (b t) -> g b t", b=GRAPHS),
            in_=node_mask.rearrange("b (g t) -> g b t", t=TILES),
        )
        node_rows = const.tile([P, FEAT], BF16)
        nc.sync.dma_start(out=node_rows[:], in_=new_node.flatten_outer_dims())

        emb_tiles = {}

        def load(c, parts=1):
            emb = emb_pool.tile([P, TILES, FEAT], BF16)
            step = TILES // parts
            for part in range(parts):
                rows = slice(part * step, (part + 1) * step)
                nc.sync.dma_start(out=emb[:, rows, :], in_=emb_chunks[c][:, rows, :])
            emb_tiles[c] = emb

        load(0, parts=2)

        w_planes = const.tile([P, 3, FEAT], U8, align_bytes=64)
        nc.vector.memset(w_planes[:].bitcast(I32), 0)
        w_words = const.tile([P, 3, 2 * FEAT], U8, align_bytes=64)
        scales_i32 = Wedge_scales.bitcast(I32)
        for quadrant in range(4):
            nc.sync.dma_start(
                out=w_planes[32 * quadrant : 32 * quadrant + 4].bitcast(I32),
                in_=scales_i32[:, 4 * quadrant : 4 * quadrant + 4, :].rearrange("g q n -> q g n"),
            )
        nc.sync.dma_start(
            out=w_words[:].bitcast(I32), in_=Wedge_words.bitcast(I32).rearrange("g p n -> p g n")
        )

        bias_rows = const.tile([P, P], BF16)
        nc.vector.memset(bias_rows[:], 0.0)
        nc.sync.dma_start(
            out=bias_rows[0:FEATURE_BLOCKS, :], in_=bedge.rearrange("(f q) -> f q", q=P)
        )
        GAMMA, BETA = 0, 1
        vectors = const.tile([P, 2, FEAT], BF16)
        nc.vector.memset(vectors[:], 0.0)
        load(1)
        nc.sync.dma_start(out=vectors[0:1, GAMMA, :], in_=gamma_e.rearrange("(o n) -> o n", o=1))
        nc.sync.dma_start(out=vectors[0:1, BETA, :], in_=beta_e.rearrange("(o n) -> o n", o=1))
        ones = const.tile([P, P], BF16)
        nc.vector.memset(ones[:], 1.0)
        identity = const.tile([P, P], F32)
        make_identity(nc, identity[:])

        table_warmer = const.tile([P, 1], F32)
        nc.scalar.activation(
            out=table_warmer[:], in_=eps[:], func=ACT.Abs_reciprocal_sqrt, bias=eps[:, 0:1], scale=1.0
        )

        first_columns = const.tile([P, J_GROUPS], BF16)
        nc.vector.tensor_copy(out=first_columns[:], in_=identity[:, 0:J_GROUPS])
        select_j = const.tile([P, I_PER_CHUNK, J_GROUPS], BF16)
        nc.vector.tensor_copy(
            out=select_j[:],
            in_=first_columns[:].unsqueeze(1).to_broadcast([P, I_PER_CHUNK, J_GROUPS]),
        )
        spread_i = const.tile([P, I_PER_CHUNK, J_GROUPS], BF16)
        nc.vector.tensor_copy(
            out=spread_i[:],
            in_=mask_rows[:].unsqueeze(2).to_broadcast([P, I_PER_CHUNK, J_GROUPS]),
        )
        mask_psum = psum_rows.tile([P, FEAT], F32, tag="by_rows")
        nc.tensor.matmul(
            out=mask_psum[:, CHUNKS : CHUNKS + GRAPHS * TILES],
            lhsT=select_j[:].rearrange("p a g -> p (a g)"),
            rhs=mask_cols[:],
            start=True,
            stop=True,
        )
        nc.tensor.matmul(
            out=mask_psum[:, 0:CHUNKS],
            lhsT=spread_i[:].rearrange("p a g -> p (a g)"),
            rhs=first_columns[:],
            start=True,
            stop=True,
        )
        mask_j = const.tile([P, GRAPHS * TILES], F32)
        nc.vector.tensor_copy(out=mask_j[:], in_=mask_psum[:, CHUNKS : CHUNKS + GRAPHS * TILES])
        e_mask = const.tile([P, CHUNKS, TILES], F32)
        nc.vector.tensor_tensor(
            out=e_mask[:].rearrange("p (b c) t -> p b c t", b=GRAPHS),
            in0=mask_psum[:, 0:CHUNKS]
            .rearrange("p (b c) -> p b c", b=GRAPHS)
            .unsqueeze(3)
            .to_broadcast([P, GRAPHS, CHUNKS_PER_GRAPH, TILES]),
            in1=mask_j[:]
            .rearrange("p (b t) -> p b t", b=GRAPHS)
            .unsqueeze(2)
            .to_broadcast([P, GRAPHS, CHUNKS_PER_GRAPH, TILES]),
            op=ALU.mult,
        )

        node_psum = psum_rows.tile([P, FEAT], F32, tag="by_rows")
        for u in range(2):
            nc.tensor.transpose(
                out=node_psum[:, u * P : (u + 1) * P],
                in_=node_rows[:].bitcast(F32)[:, u:WORDS:2],
                identity=identity[:],
            )
        node_words = node_psum[:, 0 : 2 * P].rearrange("p (u n) -> p u n", u=2)

        bias_column = const.tile([P, FEATURE_BLOCKS], F32)
        gain_shift = psum_const.tile([P, 2, FEAT], BF16)
        gamma_all = gain_shift[:, GAMMA, :]
        beta_all = gain_shift[:, BETA, :]
        gain_shift_sbuf = const.tile([P, 2, FEAT], F32)

        def spread_bias():
            bias_psum = psum_rows.tile([P, FEAT], F32, tag="by_rows")
            nc.tensor.matmul(
                out=bias_psum[:, 0:FEATURE_BLOCKS],
                lhsT=bias_rows[:],
                rhs=first_columns[:, 0:FEATURE_BLOCKS],
                start=True,
                stop=True,
            )
            nc.scalar.copy(out=bias_column[:], in_=bias_psum[:, 0:FEATURE_BLOCKS])

        def spread_gain_shift():
            for which in (GAMMA, BETA):
                nc.tensor.matmul(
                    out=gain_shift[:, which, :],
                    lhsT=ones[:],
                    rhs=vectors[:, which, :],
                    start=True,
                    stop=True,
                )

        def copy_gain_shift():
            nc.vector.tensor_copy(out=gain_shift_sbuf[:], in_=gain_shift[:])

        row_codes = const.tile([P, GRAPHS, CHUNKS_PER_GRAPH * P], U32, align_bytes=64)
        row_planes = const.tile([P, GRAPHS, CHUNKS_PER_GRAPH * P], U8, align_bytes=64)
        col_codes = const.tile([P, GRAPHS, TILES * P], U32, align_bytes=64)
        col_planes = const.tile([P, GRAPHS, TILES * P], U8, align_bytes=64)

        node_col_in = const.tile([P, GRAPHS, NODES * PACK], BF16, align_bytes=64)
        node_row_in = const.tile([P, GRAPHS, NODES * REPEATS * PACK], BF16, align_bytes=64)
        node_col_codes = const.tile([P, GRAPHS, NODES], U32, align_bytes=64)
        node_row_codes = const.tile([P, GRAPHS, NODES * REPEATS], U32, align_bytes=64)
        node_col_planes = const.tile([P, GRAPHS, NODES], U8, align_bytes=64)
        nc.vector.memset(node_col_planes[:].bitcast(I32), 0)
        node_row_planes = const.tile([P, GRAPHS, NODES * REPEATS], U8, align_bytes=64)
        nc.vector.memset(node_row_planes[:].bitcast(I32), 0)

        def copy_nodes(b):
            nc.scalar.copy(
                out=node_col_in[:, b, :].bitcast(F32).rearrange("p (t g u) -> p t g u", t=TILES, u=2),
                in_=node_words[:, :, b * NODES : (b + 1) * NODES].rearrange(
                    "p u (g t) -> p t g u", t=TILES
                ),
            )
            nc.scalar.copy(
                out=node_row_in[:, b, :].bitcast(F32).rearrange("p (n r u) -> p n r u", r=REPEATS, u=2),
                in_=node_words[:, :, b * NODES : (b + 1) * NODES]
                .rearrange("p u n -> p n u")
                .unsqueeze(2)
                .to_broadcast([P, NODES, REPEATS, 2]),
            )

        def quantise_nodes(b):
            nc.vector.quantize_mx(
                out=node_col_codes[:, b, :].bitcast(FP8X4),
                scales=node_col_planes[:, b, :],
                in_=node_col_in[:, b, :],
            )
            nc.vector.quantize_mx(
                out=node_row_codes[:, b, :].bitcast(FP8X4),
                scales=node_row_planes[:, b, :],
                in_=node_row_in[:, b, :],
            )

        def spread_col_nodes(b, copy):
            copy(
                out=col_codes[:, b, :]
                .bitcast(I32)
                .rearrange("p (t a g) -> p t a g", t=TILES, a=I_PER_CHUNK),
                in_=node_col_codes[:, b, :]
                .bitcast(I32)
                .rearrange("p (t g) -> p t g", t=TILES)
                .unsqueeze(2)
                .to_broadcast([P, TILES, I_PER_CHUNK, J_GROUPS]),
            )
            copy(
                out=col_planes[:, b, :]
                .bitcast(I32)
                .rearrange("p (t a w) -> p t a w", t=TILES, a=I_PER_CHUNK),
                in_=node_col_planes[:, b, :]
                .bitcast(I32)
                .rearrange("p (t w) -> p t w", t=TILES)
                .unsqueeze(2)
                .to_broadcast([P, TILES, I_PER_CHUNK, J_GROUPS // 4]),
            )

        def spread_row_nodes(b, first, chunks, copy):
            nodes = slice(first * I_PER_CHUNK, (first + chunks) * I_PER_CHUNK)
            cols = slice(first * P, (first + chunks) * P)
            small = slice(nodes.start * REPEATS, nodes.stop * REPEATS)
            copies = J_GROUPS // REPEATS
            copy(
                out=row_codes[:, b, cols].bitcast(I32).rearrange("p (n q r) -> p n q r", q=copies, r=REPEATS),
                in_=node_row_codes[:, b, small]
                .bitcast(I32)
                .rearrange("p (n r) -> p n r", r=REPEATS)
                .unsqueeze(2)
                .to_broadcast([P, chunks * I_PER_CHUNK, copies, REPEATS]),
            )
            copy(
                out=row_planes[:, b, cols].bitcast(I32).rearrange("p (n q) -> p n q", q=copies),
                in_=node_row_planes[:, b, small]
                .bitcast(I32)
                .unsqueeze(2)
                .to_broadcast([P, chunks * I_PER_CHUNK, copies]),
            )

        xe_tiles, xt_tiles, grouped_tiles, code_tiles, feature_tiles, edge_tiles = {}, {}, {}, {}, {}, {}
        y_tiles, minus_mean_tiles, square_tiles, rstd_tiles, scaled_tiles = {}, {}, {}, {}, {}
        squares_unread = const.tile([P, FEAT], BF16)

        def mask(j, engine, tiles=(0, 1)):
            c, half = divmod(j, 2)
            if j not in xe_tiles:
                new_xe = xe_pool.tile([P, PAIR, FEAT], BF16)
                xe_tiles[j] = new_xe
            xe = xe_tiles[j]
            for a in tiles:
                t = PAIR * half + a
                xe_words = xe[:, a, :].rearrange("p (u w e) -> p u w e", u=2, e=2) if UW else xe[:, a, :]
                emb_words = (
                    emb_tiles[c][:, t, :].rearrange("p (w u e) -> p u w e", u=2, e=2)
                    if UW
                    else emb_tiles[c][:, t, :]
                )
                if engine == "vector":
                    nc.vector.tensor_scalar_mul(
                        out=xe_words, in0=emb_words, scalar1=e_mask[:, c, t : t + 1]
                    )
                elif engine == "scalar":
                    nc.scalar.activation(
                        out=xe_words, in_=emb_words, func=ACT.Copy, scale=e_mask[:, c, t : t + 1]
                    )
                else:
                    nc.gpsimd.tensor_scalar(
                        out=xe_words,
                        in0=emb_words,
                        scalar1=e_mask[:, c, t : t + 1],
                        scalar2=1.0,
                        op0=ALU.mult,
                        op1=ALU.mult,
                    )

        def transpose(j):
            if j in (1, 3):
                free_bank = psum_rows.tile([P, FEAT], F32, tag="by_rows")
                xt = free_bank[:].rearrange("p (a u r) -> p a u r", a=PAIR, u=2)
            else:
                xt_bank = psum_xt.tile([P, PAIR, 2, P], F32, tag="xt")
                xt = xt_bank[:]
            for a in range(PAIR):
                for u in range(2):
                    nc.tensor.transpose(
                        out=xt[:, a, u, :],
                        in_=xe_tiles[j][:, a, :].bitcast(F32)[:, u * P : (u + 1) * P]
                        if UW
                        else xe_tiles[j][:, a, :].bitcast(F32)[:, u:WORDS:2],
                        identity=identity[:],
                    )
            xt_tiles[j] = xt

        def vector_regroups(j):
            return VREG and j >= 6 and j % VREG == VR

        def regroup(j):
            c, half = divmod(j, 2)
            if half == 0:
                grouped = stage.tile([P, TILES * P * PACK], BF16, align_bytes=64)
                grouped_tiles[c] = grouped
            grouped_words = (
                grouped_tiles[c][:].bitcast(F32).rearrange("p (t r u) -> p t r u", t=TILES, u=2)
            )
            copy = nc.vector.tensor_copy if vector_regroups(j) else nc.scalar.copy
            copy(
                out=grouped_words[:, PAIR * half : PAIR * half + PAIR],
                in_=xt_tiles[j].rearrange("p a u r -> p a r u"),
            )

        def quantise(c):
            codes = stage.tile([P, TILES * P], U32, align_bytes=64)
            planes = stage.tile([P, TILES * P], U8, align_bytes=64)
            nc.vector.quantize_mx(
                out=codes[:].bitcast(FP8X4), scales=planes[:], in_=grouped_tiles[c][:]
            )
            code_tiles[c] = (codes, planes)
            by_features = feature_pool.tile([P, FEATURE_BLOCKS, TILES * P], F32)
            feature_tiles[c] = by_features

        def weight(block, f):
            return {
                "lhsT": w_words[:, block, 2 * P * f : 2 * P * (f + 1)].bitcast(FP4X4),
                "lhsT_scale": w_planes[:, block, P * f : P * (f + 1)],
            }

        acc_tiles = {}

        def multiply_block(c, f):
            b, chunk_in_graph = divmod(c, CHUNKS_PER_GRAPH)
            codes, planes = code_tiles[c]
            row_cols = slice(chunk_in_graph * P, (chunk_in_graph + 1) * P)
            acc = psum_features.tile([P, TILES * P], F32)
            nc.tensor.matmul_mx(
                out=acc[:],
                rhs=codes[:].bitcast(FP8X4),
                rhs_scale=planes[:],
                start=True,
                stop=False,
                **weight(EDGE_BLOCK, f),
            )
            nc.tensor.matmul_mx(
                out=acc[:],
                rhs=col_codes[:, b, :].bitcast(FP8X4),
                rhs_scale=col_planes[:, b, :],
                start=False,
                stop=False,
                **weight(COL_BLOCK, f),
            )
            for t in range(TILES):
                nc.tensor.matmul_mx(
                    out=acc[:, t * P : (t + 1) * P],
                    rhs=row_codes[:, b, row_cols].bitcast(FP8X4),
                    rhs_scale=row_planes[:, b, row_cols],
                    start=False,
                    stop=(t == TILES - 1),
                    **weight(ROW_BLOCK, f),
                )
            acc_tiles[c, f] = acc

        def copy_block(c, f):
            nc.scalar.activation(
                out=feature_tiles[c][:, f, :],
                in_=acc_tiles[c, f][:],
                func=ACT.Identity,
                bias=bias_column[:, f : f + 1],
            )

        def to_rows(j):
            c, half = divmod(j, 2)
            for a in range(PAIR):
                t = PAIR * half + a
                by_rows = psum_rows.tile([P, FEAT], F32)
                for f in range(FEATURE_BLOCKS):
                    nc.tensor.transpose(
                        out=by_rows[:, f * P : (f + 1) * P],
                        in_=feature_tiles[c][:, f, t * P : (t + 1) * P],
                        identity=identity[:],
                    )
                edge_tiles[j, a] = by_rows

        def add_residual(j):
            c, half = divmod(j, 2)
            y = row_pool.tile([P, PAIR, FEAT], F32)
            sums = stats.tile([P, PAIR], F32)
            for a in range(PAIR):
                t = PAIR * half + a
                nc.vector.scalar_tensor_tensor(
                    out=y[:, a, :],
                    in0=emb_tiles[c][:, t, :],
                    scalar=e_mask[:, c, t : t + 1],
                    in1=edge_tiles[j, a][:],
                    op0=ALU.mult,
                    op1=ALU.add,
                    accum_out=sums[:, a : a + 1],
                )
            y_tiles[j] = (y, sums)

        def mean(j):
            minus_mean = stats.tile([P, PAIR], F32)
            nc.scalar.activation(
                out=minus_mean[:], in_=y_tiles[j][1][:], func=ACT.Copy, scale=-1.0 / FEAT
            )
            minus_mean_tiles[j] = minus_mean
            squares = stats.tile([P, PAIR], F32)
            square_tiles[j] = squares

        def on_gpsimd(j, a):
            c, t = j // 2, PAIR * (j % 2) + a
            if c == CHUNKS - 1:
                return t == GL
            if c % 4 in G2 and t == ST and GMIN <= c < GMAX:
                return True
            return t in GPSIMD_TILES

        def centre_and_gain(j):
            scaled = row_pool.tile([P, PAIR, FEAT], F32)
            for a in range(PAIR):
                if not on_gpsimd(j, a):
                    nc.vector.scalar_tensor_tensor(
                        out=scaled[:, a, :],
                        in0=y_tiles[j][0][:, a, :],
                        scalar=minus_mean_tiles[j][:, a : a + 1],
                        in1=gamma_all,
                        op0=ALU.add,
                        op1=ALU.mult,
                    )
            scaled_tiles[j] = scaled

        def sum_squares(j, a):
            nc.scalar.activation(
                out=squares_unread[:],
                in_=y_tiles[j][0][:, a, :],
                func=ACT.Square,
                bias=minus_mean_tiles[j][:, a : a + 1],
                accum_out=square_tiles[j][:, a : a + 1],
            )

        def inverse_deviation(j):
            rstd = stats.tile([P, PAIR], F32)
            nc.scalar.activation(
                out=rstd[:],
                in_=square_tiles[j][:],
                func=ACT.Abs_reciprocal_sqrt,
                bias=eps[:, 0:1],
                scale=1.0 / FEAT,
            )
            rstd_tiles[j] = rstd

        def normalise_on_gpsimd(j):
            scaled = scaled_tiles[j]
            tiles = [a for a in range(PAIR) if on_gpsimd(j, a)]
            if not tiles:
                return
            for a in tiles:
                nc.gpsimd.tensor_scalar(
                    out=scaled[:, a, :],
                    in0=y_tiles[j][0][:, a, :],
                    scalar1=minus_mean_tiles[j][:, a : a + 1],
                    scalar2=rstd_tiles[j][:, a : a + 1],
                    op0=ALU.add,
                    op1=ALU.mult,
                )
            both = scaled[:, tiles[0] : tiles[-1] + 1, :]
            for which, op in ((0, ALU.mult), (1, ALU.add)):
                nc.gpsimd.tensor_tensor(
                    out=both,
                    in0=both,
                    in1=gain_shift_sbuf[:, which, :].unsqueeze(1).to_broadcast([P, len(tiles), FEAT]),
                    op=op,
                )

        def normalise(j):
            scaled = scaled_tiles[j]
            for a in range(PAIR):
                if not on_gpsimd(j, a):
                    nc.vector.scalar_tensor_tensor(
                        out=scaled[:, a, :],
                        in0=scaled[:, a, :],
                        scalar=rstd_tiles[j][:, a : a + 1],
                        in1=beta_all,
                        op0=ALU.mult,
                        op1=ALU.add,
                    )

        def store(j, tiles=(0, 1)):
            c, half = divmod(j, 2)
            first, last = tiles[0], tiles[-1]
            nc.sync.dma_start(
                out=out_chunks[c][:, PAIR * half + first : PAIR * half + last + 1, :],
                in_=scaled_tiles[j][:, first : last + 1, :],
            )

        def pair(j):
            return 0 <= j < PAIRS

        LATE = list(range(VHEAD + GEARLY, PAIRS))
        LATE_G = [LATE[0] + GO + 2 * i for i in range(NG)]
        LATE_V = [j for j in LATE if j not in LATE_G]
        G_SLOTS = [h for h in range(7, PAIRS) if h % 2 != 0 and not (GSKIP and ((h - 5) // 2) % 4 in G2)]
        G_TILES = [(j, (a,)) for j in LATE_G for a in range(PAIR)] if GT == 1 else [(j, (0, 1)) for j in LATE_G]

        def vector_masks(h):
            if 0 <= h <= 1:
                return [j for j in range(4 + 4 * h, 8 + 4 * h) if j < VHEAD]
            if h == 2:
                return list(range(12, VHEAD))
            if h >= V0 and h % 2 != 0:
                return LATE_V[(h - V0) // 2 : (h - V0) // 2 + 1]
            return []

        def gpsimd_masks(h):
            if 0 <= h < GEARLY:
                return [(VHEAD + h, (0, 1))]
            if h in G_SLOTS:
                return G_TILES[G_SLOTS.index(h) : G_SLOTS.index(h) + 1]
            return []

        LOAD_LEAD = 17
        EMB_BUFFERS = 11
        for c in range(2, EMB_BUFFERS):
            load(c)

        mask(0, "vector")
        copy_nodes(0)
        transpose(0)
        mask(1, "vector")
        transpose(1)
        regroup(0)
        quantise_nodes(0)
        spread_col_nodes(0, nc.vector.tensor_copy)
        spread_row_nodes(0, 0, 2, nc.vector.tensor_copy)
        regroup(1)
        quantise(0)
        copy_nodes(1)
        spread_row_nodes(0, 2, 6, nc.vector.tensor_copy)
        mask(2, "vector")
        mask(3, "vector")
        quantise_nodes(1)
        spread_col_nodes(1, nc.vector.tensor_copy)
        spread_row_nodes(1, 0, CHUNKS_PER_GRAPH, nc.vector.tensor_copy)

        for h in range(-LOAD_LEAD, PAIRS + 6):
            if h % 2 != 0 and EMB_BUFFERS <= (h + LOAD_LEAD) // 2 < CHUNKS:
                load((h + LOAD_LEAD) // 2)
            if ML == 1 and pair(h - 4):
                mean(h - 4)
            if h >= 1 and pair(h + 2):
                regroup(h + 2)
            if ML == 2 and pair(h - 4):
                mean(h - 4)
            if h >= QF:
                if h % 2 != 0 and pair(h + 1):
                    quantise((h + 1) // 2)
                for j in vector_masks(h):
                    mask(j, "vector")
            if pair(h - 3):
                add_residual(h - 3)
            if h == GH:
                copy_gain_shift()
            first_block = 2 * (h % 2)
            rows_first = h in (2, 3)
            if rows_first:
                to_rows(h - 2)
            if pair(h):
                multiply_block(h // 2, first_block)
            if h == 0:
                spread_bias()
            if ML != 3 and pair(h - 4):
                sum_squares(h - 4, 0)
            if pair(h):
                copy_block(h // 2, first_block)
                multiply_block(h // 2, first_block + 1)
            if ML == 3 and pair(h - 4):
                mean(h - 4)
                sum_squares(h - 4, 0)
            if pair(h - 4):
                sum_squares(h - 4, 1)
                if not IL:
                    inverse_deviation(h - 4)
            if pair(h):
                copy_block(h // 2, first_block + 1)
            if IL and pair(h - 4):
                inverse_deviation(h - 4)
            if ML == 0 and pair(h - 3):
                mean(h - 3)
            if h < QF:
                if h >= 0 and h % 2 != 0 and pair(h + 1):
                    quantise((h + 1) // 2)
                for j in vector_masks(h):
                    mask(j, "vector")
            if pair(h - 4):
                centre_and_gain(h - 4)
            if pair(h - 5):
                normalise(h - 5)
            if pair(h - 2) and not rows_first:
                to_rows(h - 2)
            if h == 0:
                transpose(2)
                regroup(2)
            if h >= 0 and pair(h + 3):
                transpose(h + 3)
            if h == 1:
                spread_gain_shift()
            if h % 2 != 0:
                for j in (h - 5, h - 4):
                    if pair(j):
                        normalise_on_gpsimd(j)
            if pair(h - 5) and h - 5 < PAIRS - 2:
                store(h - 5)
            if h - 5 == PAIRS - 2:
                store(PAIRS - 2, (0,))
            if h - 5 == PAIRS - 1:
                store(PAIRS - 1, (0,))
                store(PAIRS - 1, (1,))
                store(PAIRS - 2, (1,))
            for j, tiles in gpsimd_masks(h):
                mask(j, "gpsimd", tiles)
